import numpy as np
import ml_dtypes


def mxq(x, axis, fmt="e4m3"):
    dtype, down = {"e4m3": (ml_dtypes.float8_e4m3fn, 7), "e5m2": (ml_dtypes.float8_e5m2, 14)}[fmt]
    v = np.moveaxis(np.asarray(x, np.float32).astype(ml_dtypes.bfloat16).astype(np.float64), axis, -1)
    blocks = v.reshape(v.shape[:-1] + (-1, 32))
    amax = np.abs(blocks).max(-1, keepdims=True)
    byte = np.maximum(np.where(amax > 0, np.frexp(amax)[1] - 1 + 127, 0) - down, 1)
    scale = np.exp2(byte - 127.0)
    codes = (blocks / scale).astype(np.float32).astype(dtype).astype(np.float64)
    return np.moveaxis((codes * scale).reshape(v.shape), -1, axis)


WIDE = False


def mx_kscale(k):
    if not WIDE:
        return np.ones(k)
    levels = np.array([10, -10, 5, -5, 0])
    a = np.random.permutation(np.resize(levels, k // 512 * 4)).reshape(k // 512, 4)
    idx = np.arange(k)
    return np.exp2(a[idx // 512, idx % 128 // 32])


BF16 = ml_dtypes.bfloat16


def bf(x):
    return np.asarray(x, np.float32).astype(BF16)


def f64(x):
    return np.asarray(x).astype(np.float64)


N, IN_DIM, HID, NUM_CLASSES, AVG_DEG = 2048, 512, 512, 512, 32


def setup_inputs():
    s = mx_kscale(IN_DIM)
    edges = np.random.uniform(size=(N, N)) < AVG_DEG / N
    return {"A": bf(edges * (0.5 + np.random.uniform(size=(N, N)))),
            "x": bf(np.random.standard_normal((N, IN_DIM)) * 0.5 * s),
            "W1": bf(np.random.standard_normal((IN_DIM, HID)) * 4.0 / np.sqrt(IN_DIM) / s[:, None]),
            "b1": bf(np.random.standard_normal(HID) * 0.1)}


def reference(A, x, W1, b1):
    A = f64(A)
    deg = A.sum(0) + 1.0
    dis = (1.0 / np.sqrt(deg))[:, None]
    h = mxq(f64(x), 1, "e4m3") @ mxq(f64(W1), 0, "e4m3")
    m = dis * h
    agg = mxq(A, 0, "e4m3").T @ mxq(m, 0, "e4m3")
    return np.maximum(dis * agg + dis ** 2 * h + f64(b1), 0.0)

@@ -1,0 +1,337 @@
+from contextlib import ExitStack
+
+import concourse.mybir as mybir
+from concourse.masks import make_identity
+
+BF16 = mybir.dt.bfloat16
+F32 = mybir.dt.float32
+U32 = mybir.dt.uint32
+U8 = mybir.dt.uint8
+FP8X4 = mybir.dt.float8_e4m3fn_x4
+ACT = mybir.ActivationFunctionType
+ALU = mybir.AluOpType
+AXIS = mybir.AxisListType
+
+P = 128
+NODES = 2048
+FEAT = 512
+UNIT = 2048
+K_SLOTS = 9
+
+FLOPS = 2 * NODES * FEAT * FEAT + 2 * NODES * NODES * FEAT
+
+LOADS = (("a", 0), ("a", 1), ("W", 0), ("x", 0), ("a", 2), ("x", 1), ("a", 3), ("x", 2), ("a", 4), ("x", 3), ("a", 5), ("a", 6), ("a", 7), ("a", 8), ("a", 9), ("a", 10), ("a", 11), ("a", 12), ("a", 13), ("a", 14), ("a", 15))
+
+ORDER = (
+    ("R", 0, "V"), ("Q", 0, "V"), ("deg", 1, "PE"), ("R", 1, "S"), ("pbm", 0, "PE"),
+    ("deg", 0, "PE"), ("Wr", 0, "V"), ("pbc", 0, "S"), ("Wq", 0, "V"), ("tr", 0, "PE"),
+    ("tr", 1, "PE"), ("Q", 1, "V"), ("xc", 0, "S"), ("xc", 1, "S"), ("deg", 2, "PE"),
+    ("R", 2, "V"), ("xq", 0, "V"), ("tr", 3, "PE"), ("tr", 2, "PE"), ("Q", 2, "V"),
+    ("xc", 3, "S"), ("xc", 2, "S"), ("deg", 3, "PE"), ("R", 3, "V"), ("h", 3, "PE"),
+    ("red", 0, "V"), ("Q", 3, "V"), ("tr", 4, "PE"), ("sq", 0, "S"), ("h", 0, "PE"),
+    ("xq", 1, "V"), ("xc", 4, "S"), ("h", 1, "PE"), ("h", 2, "PE"), ("rec", 0, "V"),
+    ("deg", 4, "PE"), ("R", 4, "V"), ("mf", 0, "S"), ("h", 5, "PE"), ("mf", 3, "S"),
+    ("s", 0, "V"), ("tr", 6, "PE"), ("mf", 2, "S"), ("h", 7, "PE"), ("s", 3, "V"),
+    ("tr", 5, "PE"), ("mf", 1, "S"), ("Q", 4, "V"), ("h", 6, "PE"), ("tr", 7, "PE"),
+    ("xc", 6, "S"), ("R", 5, "V"), ("deg", 5, "PE"), ("xc", 5, "S"), ("xc", 7, "S"),
+    ("deg", 6, "PE"), ("mg", 0, "V"), ("R", 6, "S"), ("Q", 5, "V"), ("deg", 7, "PE"),
+    ("xq", 3, "V"), ("R", 7, "V"), ("deg", 8, "PE"), ("R", 8, "S"), ("h", 4, "PE"),
+    ("qm", 0, "V"), ("deg", 9, "PE"), ("red", 1, "V"), ("Q", 7, "V"), ("xq", 2, "V"),
+    ("sq", 1, "S"), ("R", 9, "S"), ("s", 2, "V"), ("h", 8, "PE"), ("deg", 10, "PE"),
+    ("Q", 6, "V"), ("rec", 1, "V"), ("deg", 11, "PE"), ("R", 10, "V"), ("mf", 7, "S"),
+    ("h", 12, "PE"), ("h", 10, "PE"), ("Q", 9, "V"), ("mf", 4, "S"), ("deg", 12, "PE"),
+    ("Q", 8, "V"), ("mf", 5, "S"), ("s", 1, "V"), ("deg", 13, "PE"), ("mf", 6, "S"),
+    ("red", 2, "V"), ("s", 7, "V"), ("h", 9, "PE"), ("sq", 2, "S"), ("s", 5, "V"),
+    ("R", 11, "S"), ("deg", 14, "PE"), ("mg", 1, "V"), ("h", 11, "PE"), ("deg", 15, "PE"),
+    ("rec", 2, "V"), ("s", 6, "V"), ("mf", 10, "S"), ("qm", 1, "V"), ("mf", 9, "S"),
+    ("s", 10, "V"), ("p", 5, "PE"), ("mf", 8, "S"), ("h", 13, "PE"), ("red", 3, "V"),
+    ("s", 4, "V"), ("h", 14, "PE"), ("p", 9, "PE"), ("sq", 3, "S"), ("Q", 11, "V"),
+    ("h", 15, "PE"), ("mf", 11, "S"), ("p", 1, "PE"), ("p", 0, "PE"), ("rec", 3, "V"),
+    ("s", 8, "V"), ("mf", 15, "S"), ("p", 29, "PE"), ("mg", 2, "V"), ("mf", 13, "S"),
+    ("p", 24, "PE"), ("p", 25, "PE"), ("mf", 12, "S"), ("p", 8, "PE"), ("Q", 10, "V"),
+    ("p", 12, "PE"), ("p", 28, "PE"), ("mf", 14, "S"), ("qm", 2, "V"), ("p", 13, "PE"),
+    ("R", 14, "S"), ("s", 9, "V"), ("p", 10, "PE"), ("p", 20, "PE"), ("mg", 3, "V"),
+    ("p", 18, "PE"), ("p", 17, "PE"), ("p", 14, "PE"), ("p", 16, "PE"), ("qm", 3, "V"),
+    ("p", 6, "PE"), ("R", 13, "S"), ("p", 2, "PE"), ("s", 13, "V"), ("p", 19, "PE"),
+    ("p", 3, "PE"), ("s", 12, "V"), ("p", 30, "PE"), ("p", 15, "PE"), ("ep", 4, "V"),
+    ("p", 11, "PE"), ("p", 21, "PE"), ("Q", 14, "V"), ("R", 15, "S"), ("p", 34, "PE"),
+    ("p", 27, "PE"), ("s", 11, "V"), ("p", 23, "PE"), ("p", 26, "PE"), ("ep", 2, "V"),
+    ("p", 31, "PE"), ("p", 7, "PE"), ("Q", 13, "V"), ("p", 22, "PE"), ("p", 39, "PE"),
+    ("R", 12, "S"), ("ep", 7, "V"), ("p", 36, "PE"), ("p", 32, "PE"), ("ep", 0, "V"),
+    ("p", 54, "PE"), ("p", 4, "PE"), ("ep", 3, "V"), ("p", 44, "PE"), ("p", 37, "PE"),
+    ("ep", 1, "V"), ("p", 40, "PE"), ("rl", 0, "S"), ("p", 33, "PE"), ("ep", 5, "V"),
+    ("p", 45, "PE"), ("rl", 7, "S"), ("p", 53, "PE"), ("ep", 6, "V"), ("p", 38, "PE"),
+    ("rl", 1, "S"), ("p", 42, "PE"), ("Q", 15, "V"), ("p", 41, "PE"), ("rl", 4, "S"),
+    ("p", 47, "PE"), ("Q", 12, "V"), ("p", 46, "PE"), ("p", 35, "PE"), ("rl", 2, "S"),
+    ("ep", 9, "V"), ("p", 43, "PE"), ("p", 61, "PE"), ("rl", 6, "S"), ("ep", 8, "V"),
+    ("p", 55, "PE"), ("p", 56, "PE"), ("rl", 9, "S"), ("p", 59, "PE"), ("ep", 10, "V"),
+    ("p", 50, "PE"), ("rl", 5, "S"), ("p", 52, "PE"), ("s", 14, "V"), ("p", 49, "PE"),
+    ("rl", 3, "S"), ("p", 51, "PE"), ("ep", 11, "V"), ("p", 58, "PE"), ("rl", 8, "S"),
+    ("p", 48, "PE"), ("ep", 13, "V"), ("p", 60, "PE"), ("rl", 11, "S"), ("p", 63, "PE"),
+    ("s", 15, "V"), ("p", 62, "PE"), ("rl", 13, "S"), ("p", 57, "PE"), ("ep", 12, "V"),
+    ("rl", 10, "S"), ("ep", 14, "V"), ("rl", 12, "S"), ("ep", 15, "V"), ("rl", 14, "S"),
+    ("rl", 15, "V"),
+)
+
+
+def tile_gcnnodeclassifiernetwork_pa_kernel(tc, A, x, W1, b1, out):
+    nc = tc.nc
+    with ExitStack() as ctx:
+        ctx.enter_context(tc.manual_schedule())
+        const = ctx.enter_context(tc.tile_pool(name="const", bufs=1))
+        keep = ctx.enter_context(tc.tile_pool(name="keep", bufs=1))
+        raw = ctx.enter_context(tc.tile_pool(name="raw", bufs=1))
+        kpool = ctx.enter_context(tc.tile_pool(name="kpool", bufs=1))
+        mpool = ctx.enter_context(tc.tile_pool(name="mpool", bufs=1))
+        psum = ctx.enter_context(tc.psum_pool(name="psum", bufs=1))
+
+        free = {"b": list(range(8)), "k": list(range(K_SLOTS)), "m": [0, 1]}
+        tiles = {}
+        slot_of = {}
+        readers = {}
+
+        def grab(pool, name, n_readers):
+            if name in tiles:
+                return tiles[name]
+            assert free[pool], name
+            idx = free[pool].pop(0)
+            slot_of[name] = (pool, idx)
+            readers[name] = n_readers
+            if pool == "b":
+                t = psum.tile([P, FEAT], F32, tag="b%d" % idx, name=name)
+            elif pool == "k":
+                t = kpool.tile([P, UNIT], BF16, tag="k%d" % idx, name=name, align_bytes=64)
+            else:
+                t = mpool.tile([P, 4, FEAT], F32, tag="m%d" % idx, name=name)
+            tiles[name] = t
+            return t
+
+        def drop(name):
+            readers[name] -= 1
+            if readers[name] == 0:
+                pool, idx = slot_of[name]
+                free[pool].append(idx)
+
+        def grouped(tile_ap):
+            return tile_ap.rearrange("p (c i t) -> p c t i", i=4, t=4)
+
+        def planes(tile_ap):
+            return tile_ap.rearrange("p (t c i) -> p c t i", t=4, i=4)
+
+        def copy_on(eng, dst, src):
+            if eng == "V":
+                nc.vector.tensor_copy(out=dst, in_=src)
+            else:
+                nc.scalar.copy(out=dst, in_=src)
+
+        ident = const.tile([P, P], F32, name="ident")
+        make_identity(nc, ident[:])
+        ones_bf = const.tile([P, P], BF16, name="ones_bf")
+        nc.vector.memset(ones_bf[:], 1.0)
+        one_f = const.tile([P, 1], F32, name="one_f")
+        nc.vector.memset(one_f[:], 1.0)
+        brow = const.tile([P, FEAT], BF16, name="brow")
+        nc.vector.memset(brow[:], 0.0)
+        nc.scalar.dma_start(out=brow[0:1, :], in_=b1.rearrange("(o c) -> o c", o=1))
+        junk = const.tile([P, 1], F32, name="junk")
+        nc.scalar.activation(out=junk[:], in_=one_f[:], func=ACT.Sqrt)
+        b_bc = const.tile([P, FEAT], F32, name="b_bc")
+
+        x_view = x.rearrange("(T p) k -> p T k", p=P)
+        a_view = A.rearrange("(g t p) j -> g p t j", t=4, p=P)
+        araw = {}
+        grab("k", "wraw", 1)
+        for q in range(4):
+            grab("k", "xraw%d" % q, 2)
+        for what, n in LOADS:
+            if what == "W":
+                nc.sync.dma_start(
+                    out=tiles["wraw"][:].rearrange("q (u r) -> q u r", u=2),
+                    in_=W1.rearrange("(u q e) c -> q u (e c)", u=2, q=P, e=2),
+                )
+            elif what == "x":
+                nc.sync.dma_start(
+                    out=tiles["xraw%d" % n][:].rearrange("p (T k) -> p T k", T=4),
+                    in_=x_view[:, 4 * n : 4 * n + 4, :],
+                )
+            else:
+                b, g = divmod(n, 4)
+                ar = raw.tile([P, UNIT], BF16, name="araw%d" % n)
+                nc.sync.dma_start(
+                    out=ar[:].rearrange("p (t j) -> p t j", t=4),
+                    in_=a_view[g, :, :, FEAT * b : FEAT * b + FEAT],
+                )
+                araw[n] = ar
+
+        codes = {}
+        scales = {}
+
+        def quantise(name, src):
+            cq = keep.tile([P, FEAT], U32, name="c_" + name, align_bytes=64)
+            sq = keep.tile([P, FEAT], U8, name="s_" + name, align_bytes=64)
+            nc.vector.quantize_mx(out=cq[:].bitcast(FP8X4), scales=sq[:], in_=src)
+            codes[name] = cq
+            scales[name] = sq
+
+        small = {}
+        s_tiles = {}
+        n_pass = {}
+
+        for kind, n, eng in ORDER:
+            if kind == "Wr":
+                wg = grab("k", "wg", 1)
+                nc.vector.tensor_copy(out=grouped(wg[:]), in_=planes(tiles["wraw"][:]))
+                drop("wraw")
+            elif kind == "Wq":
+                quantise("w", tiles["wg"][:])
+                drop("wg")
+            elif kind == "pbm":
+                pb = grab("b", "pb", 1)
+                nc.tensor.matmul(out=pb[:], lhsT=ones_bf[:], rhs=brow[:], start=True, stop=True)
+            elif kind == "pbc":
+                copy_on(eng, b_bc[:], tiles["pb"][:])
+                drop("pb")
+            elif kind == "tr":
+                q, hh = divmod(n, 2)
+                tp = grab("b", "tp%d" % n, 1)
+                xw = tiles["xraw%d" % q][:].bitcast(F32)
+                for tl in range(2):
+                    for u in range(2):
+                        col = 256 * (2 * hh + tl) + P * u
+                        dst = P * (2 * tl + u)
+                        nc.tensor.transpose(
+                            out=tp[:, dst : dst + P], in_=xw[:, col : col + P], identity=ident[:]
+                        )
+                drop("xraw%d" % q)
+            elif kind == "xc":
+                q, hh = divmod(n, 2)
+                xg = grab("k", "xg%d" % q, 1)
+                dstv = xg[:].bitcast(F32)[:, 512 * hh : 512 * hh + 512].rearrange(
+                    "p (T r u) -> p T r u", T=2, u=2
+                )
+                srcv = tiles["tp%d" % n][:].rearrange("p (T u r) -> p T r u", T=2, u=2)
+                copy_on(eng, dstv, srcv)
+                drop("tp%d" % n)
+            elif kind == "xq":
+                quantise("x%d" % n, tiles["xg%d" % n][:])
+                drop("xg%d" % n)
+            elif kind == "deg":
+                b, g = divmod(n, 4)
+                dg = grab("b", "dg%d" % b, 1)
+                for jl in range(4):
+                    for t in range(4):
+                        col = 16 * jl + 4 * g + t
+                        src = FEAT * t + P * jl
+                        nc.tensor.matmul(
+                            out=dg[:, col : col + 1],
+                            lhsT=araw[n][:, src : src + P],
+                            rhs=ones_bf[:, 0:1],
+                            start=True,
+                            stop=True,
+                        )
+            elif kind == "red":
+                deg = const.tile([P, 4], F32, name="deg%d" % n)
+                nc.vector.tensor_reduce(
+                    out=deg[:],
+                    in_=tiles["dg%d" % n][:, 0:64].rearrange("p (j r) -> p j r", r=16),
+                    axis=AXIS.X,
+                    op=ALU.add,
+                )
+                small["deg%d" % n] = deg
+                drop("dg%d" % n)
+            elif kind == "sq":
+                rd = const.tile([P, 4], F32, name="rd%d" % n)
+                nc.scalar.activation(
+                    out=rd[:], in_=small["deg%d" % n][:], func=ACT.Sqrt, bias=one_f[:, 0:1], scale=1.0
+                )
+                small["rd%d" % n] = rd
+            elif kind == "rec":
+                d = const.tile([P, 4], F32, name="d%d" % n)
+                nc.vector.reciprocal(out=d[:], in_=small["rd%d" % n][:])
+                small["d%d" % n] = d
+            elif kind == "h":
+                b, t = divmod(n, 4)
+                hp = grab("b", "hp%d" % n, 1)
+                nc.tensor.matmul_mx(
+                    out=hp[:],
+                    lhsT=codes["x%d" % b][:, P * t : P * t + P].bitcast(FP8X4),
+                    lhsT_scale=scales["x%d" % b][:, P * t : P * t + P],
+                    rhs=codes["w"][:].bitcast(FP8X4),
+                    rhs_scale=scales["w"][:],
+                    start=True,
+                    stop=True,
+                )
+            elif kind == "mf":
+                b, t = divmod(n, 4)
+                mf = grab("m", "mf%d" % b, 5)
+                dcol = small["d%d" % b][:, t : t + 1]
+                if eng == "S":
+                    nc.scalar.activation(
+                        out=mf[:, t, :], in_=tiles["hp%d" % n][:], func=ACT.Copy, scale=dcol
+                    )
+                else:
+                    nc.vector.tensor_scalar_mul(out=mf[:, t, :], in0=tiles["hp%d" % n][:], scalar1=dcol)
+                drop("hp%d" % n)
+            elif kind == "mg":
+                mg = grab("k", "mg%d" % n, 1)
+                nc.vector.tensor_copy(
+                    out=grouped(mg[:]), in_=tiles["mf%d" % n][:].rearrange("p t (c i) -> p c t i", i=4)
+                )
+                drop("mf%d" % n)
+            elif kind == "qm":
+                quantise("m%d" % n, tiles["mg%d" % n][:])
+                drop("mg%d" % n)
+            elif kind == "s":
+                b, t = divmod(n, 4)
+                st = keep.tile([P, FEAT], F32, name="s%d" % n)
+                nc.vector.scalar_tensor_tensor(
+                    out=st[:],
+                    in0=tiles["mf%d" % b][:, t, :],
+                    scalar=small["d%d" % b][:, t : t + 1],
+                    in1=b_bc[:],
+                    op0=ALU.mult,
+                    op1=ALU.add,
+                )
+                s_tiles[n] = st
+                drop("mf%d" % b)
+            elif kind == "R":
+                ag = grab("k", "ag%d" % n, 1)
+                copy_on(eng, grouped(ag[:]), planes(araw[n][:]))
+            elif kind == "Q":
+                quantise("a%d" % n, tiles["ag%d" % n][:])
+                drop("ag%d" % n)
+            elif kind == "p":
+                jt, c = divmod(n, 4)
+                acc = grab("b", "acc%d" % jt, 1)
+                k = n_pass.get(jt, 0)
+                n_pass[jt] = k + 1
+                name = "a%d" % (4 * (jt // 4) + c)
+                col = P * (jt % 4)
+                nc.tensor.matmul_mx(
+                    out=acc[:],
+                    lhsT=codes[name][:, col : col + P].bitcast(FP8X4),
+                    lhsT_scale=scales[name][:, col : col + P],
+                    rhs=codes["m%d" % c][:].bitcast(FP8X4),
+                    rhs_scale=scales["m%d" % c][:],
+                    start=(k == 0),
+                    stop=(k == 3),
+                )
+            elif kind == "ep":
+                st = s_tiles[n]
+                nc.vector.scalar_tensor_tensor(
+                    out=st[:],
+                    in0=tiles["acc%d" % n][:],
+                    scalar=small["d%d" % (n // 4)][:, n % 4 : n % 4 + 1],
+                    in1=st[:],
+                    op0=ALU.mult,
+                    op1=ALU.add,
+                )
+                drop("acc%d" % n)
+            else:
+                assert kind == "rl"
+                st = s_tiles[n]
+                if eng == "S":
+                    nc.scalar.activation(out=st[:], in_=st[:], func=ACT.Relu)
+                else:
+                    nc.vector.tensor_scalar_max(out=st[:], in0=st[:], scalar1=0.0)
+                nc.sync.dma_start(out=out[P * n : P * n + P, :], in_=st[:])

@@ -23,53 +23,53 @@ FLOPS = 2 * NODES * FEAT * FEAT + 2 * NODES * NODES * FEAT
 LOADS = (("a", 0), ("a", 1), ("W", 0), ("x", 0), ("a", 2), ("x", 1), ("a", 3), ("x", 2), ("a", 4), ("x", 3), ("a", 5), ("a", 6), ("a", 7), ("a", 8), ("a", 9), ("a", 10), ("a", 11), ("a", 12), ("a", 13), ("a", 14), ("a", 15))
 
 ORDER = (
-    ("R", 0, "V"), ("Q", 0, "V"), ("deg", 1, "PE"), ("R", 1, "S"), ("pbm", 0, "PE"),
-    ("deg", 0, "PE"), ("Wr", 0, "V"), ("pbc", 0, "S"), ("Wq", 0, "V"), ("tr", 0, "PE"),
-    ("tr", 1, "PE"), ("Q", 1, "V"), ("xc", 0, "S"), ("xc", 1, "S"), ("deg", 2, "PE"),
-    ("R", 2, "V"), ("xq", 0, "V"), ("tr", 3, "PE"), ("tr", 2, "PE"), ("Q", 2, "V"),
-    ("xc", 3, "S"), ("xc", 2, "S"), ("deg", 3, "PE"), ("R", 3, "V"), ("h", 3, "PE"),
-    ("red", 0, "V"), ("Q", 3, "V"), ("tr", 4, "PE"), ("sq", 0, "S"), ("h", 0, "PE"),
-    ("xq", 1, "V"), ("xc", 4, "S"), ("h", 1, "PE"), ("h", 2, "PE"), ("rec", 0, "V"),
-    ("deg", 4, "PE"), ("R", 4, "V"), ("mf", 0, "S"), ("h", 5, "PE"), ("mf", 3, "S"),
-    ("s", 0, "V"), ("tr", 6, "PE"), ("mf", 2, "S"), ("h", 7, "PE"), ("s", 3, "V"),
-    ("tr", 5, "PE"), ("mf", 1, "S"), ("Q", 4, "V"), ("h", 6, "PE"), ("tr", 7, "PE"),
-    ("xc", 6, "S"), ("R", 5, "V"), ("deg", 5, "PE"), ("xc", 5, "S"), ("xc", 7, "S"),
-    ("deg", 6, "PE"), ("mg", 0, "V"), ("R", 6, "S"), ("Q", 5, "V"), ("deg", 7, "PE"),
-    ("xq", 3, "V"), ("R", 7, "V"), ("deg", 8, "PE"), ("R", 8, "S"), ("h", 4, "PE"),
-    ("qm", 0, "V"), ("deg", 9, "PE"), ("red", 1, "V"), ("Q", 7, "V"), ("xq", 2, "V"),
-    ("sq", 1, "S"), ("R", 9, "S"), ("s", 2, "V"), ("h", 8, "PE"), ("deg", 10, "PE"),
-    ("Q", 6, "V"), ("rec", 1, "V"), ("deg", 11, "PE"), ("R", 10, "V"), ("mf", 7, "S"),
-    ("h", 12, "PE"), ("h", 10, "PE"), ("Q", 9, "V"), ("mf", 4, "S"), ("deg", 12, "PE"),
-    ("Q", 8, "V"), ("mf", 5, "S"), ("s", 1, "V"), ("deg", 13, "PE"), ("mf", 6, "S"),
-    ("red", 2, "V"), ("s", 7, "V"), ("h", 9, "PE"), ("sq", 2, "S"), ("s", 5, "V"),
-    ("R", 11, "S"), ("deg", 14, "PE"), ("mg", 1, "V"), ("h", 11, "PE"), ("deg", 15, "PE"),
-    ("rec", 2, "V"), ("s", 6, "V"), ("mf", 10, "S"), ("qm", 1, "V"), ("mf", 9, "S"),
-    ("s", 10, "V"), ("p", 5, "PE"), ("mf", 8, "S"), ("h", 13, "PE"), ("red", 3, "V"),
-    ("s", 4, "V"), ("h", 14, "PE"), ("p", 9, "PE"), ("sq", 3, "S"), ("Q", 11, "V"),
-    ("h", 15, "PE"), ("mf", 11, "S"), ("p", 1, "PE"), ("p", 0, "PE"), ("rec", 3, "V"),
-    ("s", 8, "V"), ("mf", 15, "S"), ("p", 29, "PE"), ("mg", 2, "V"), ("mf", 13, "S"),
-    ("p", 24, "PE"), ("p", 25, "PE"), ("mf", 12, "S"), ("p", 8, "PE"), ("Q", 10, "V"),
-    ("p", 12, "PE"), ("p", 28, "PE"), ("mf", 14, "S"), ("qm", 2, "V"), ("p", 13, "PE"),
-    ("R", 14, "S"), ("s", 9, "V"), ("p", 10, "PE"), ("p", 20, "PE"), ("mg", 3, "V"),
-    ("p", 18, "PE"), ("p", 17, "PE"), ("p", 14, "PE"), ("p", 16, "PE"), ("qm", 3, "V"),
-    ("p", 6, "PE"), ("R", 13, "S"), ("p", 2, "PE"), ("s", 13, "V"), ("p", 19, "PE"),
-    ("p", 3, "PE"), ("s", 12, "V"), ("p", 30, "PE"), ("p", 15, "PE"), ("ep", 4, "V"),
-    ("p", 11, "PE"), ("p", 21, "PE"), ("Q", 14, "V"), ("R", 15, "S"), ("p", 34, "PE"),
-    ("p", 27, "PE"), ("s", 11, "V"), ("p", 23, "PE"), ("p", 26, "PE"), ("ep", 2, "V"),
-    ("p", 31, "PE"), ("p", 7, "PE"), ("Q", 13, "V"), ("p", 22, "PE"), ("p", 39, "PE"),
-    ("R", 12, "S"), ("ep", 7, "V"), ("p", 36, "PE"), ("p", 32, "PE"), ("ep", 0, "V"),
-    ("p", 54, "PE"), ("p", 4, "PE"), ("ep", 3, "V"), ("p", 44, "PE"), ("p", 37, "PE"),
-    ("ep", 1, "V"), ("p", 40, "PE"), ("rl", 0, "S"), ("p", 33, "PE"), ("ep", 5, "V"),
-    ("p", 45, "PE"), ("rl", 7, "S"), ("p", 53, "PE"), ("ep", 6, "V"), ("p", 38, "PE"),
-    ("rl", 1, "S"), ("p", 42, "PE"), ("Q", 15, "V"), ("p", 41, "PE"), ("rl", 4, "S"),
-    ("p", 47, "PE"), ("Q", 12, "V"), ("p", 46, "PE"), ("p", 35, "PE"), ("rl", 2, "S"),
-    ("ep", 9, "V"), ("p", 43, "PE"), ("p", 61, "PE"), ("rl", 6, "S"), ("ep", 8, "V"),
-    ("p", 55, "PE"), ("p", 56, "PE"), ("rl", 9, "S"), ("p", 59, "PE"), ("ep", 10, "V"),
-    ("p", 50, "PE"), ("rl", 5, "S"), ("p", 52, "PE"), ("s", 14, "V"), ("p", 49, "PE"),
-    ("rl", 3, "S"), ("p", 51, "PE"), ("ep", 11, "V"), ("p", 58, "PE"), ("rl", 8, "S"),
-    ("p", 48, "PE"), ("ep", 13, "V"), ("p", 60, "PE"), ("rl", 11, "S"), ("p", 63, "PE"),
-    ("s", 15, "V"), ("p", 62, "PE"), ("rl", 13, "S"), ("p", 57, "PE"), ("ep", 12, "V"),
-    ("rl", 10, "S"), ("ep", 14, "V"), ("rl", 12, "S"), ("ep", 15, "V"), ("rl", 14, "S"),
+    ("R", 0, "V"), ("deg", 1, "PE"), ("R", 1, "S"), ("Q", 0, "V"), ("pbm", 0, "PE"),
+    ("deg", 0, "PE"), ("Wr", 0, "V"), ("tr", 1, "PE"), ("Wq", 0, "V"), ("tr", 0, "PE"),
+    ("Q", 1, "V"), ("xc", 1, "S"), ("deg", 2, "PE"), ("R", 2, "V"), ("xc", 0, "S"),
+    ("tr", 3, "PE"), ("Q", 2, "V"), ("tr", 2, "PE"), ("xq", 0, "V"), ("xc", 3, "S"),
+    ("deg", 3, "PE"), ("R", 3, "V"), ("xc", 2, "S"), ("pbc", 0, "S"), ("tr", 5, "PE"),
+    ("red", 0, "V"), ("xq", 1, "V"), ("tr", 4, "PE"), ("sq", 0, "S"), ("Q", 3, "V"),
+    ("xc", 5, "S"), ("h", 3, "PE"), ("h", 1, "PE"), ("rec", 0, "V"), ("xc", 4, "S"),
+    ("R", 4, "V"), ("mf", 1, "S"), ("tr", 7, "PE"), ("mf", 3, "S"), ("xq", 2, "V"),
+    ("h", 4, "PE"), ("h", 2, "PE"), ("xc", 7, "S"), ("Q", 4, "V"), ("h", 6, "PE"),
+    ("h", 0, "PE"), ("mf", 2, "S"), ("deg", 5, "PE"), ("s", 1, "V"), ("h", 5, "PE"),
+    ("mf", 0, "S"), ("deg", 6, "PE"), ("s", 3, "V"), ("R", 6, "S"), ("R", 5, "V"),
+    ("deg", 7, "PE"), ("deg", 4, "PE"), ("tr", 6, "PE"), ("s", 2, "V"), ("R", 7, "V"),
+    ("deg", 8, "PE"), ("h", 7, "PE"), ("R", 8, "S"), ("h", 8, "PE"), ("Q", 5, "V"),
+    ("Q", 6, "V"), ("red", 1, "V"), ("mg", 0, "V"), ("h", 10, "PE"), ("sq", 1, "S"),
+    ("R", 9, "S"), ("deg", 11, "PE"), ("deg", 10, "PE"), ("s", 0, "V"), ("deg", 9, "PE"),
+    ("qm", 0, "V"), ("rec", 1, "V"), ("Q", 8, "V"), ("xc", 6, "S"), ("R", 10, "V"),
+    ("mf", 5, "S"), ("h", 9, "PE"), ("mf", 6, "S"), ("xq", 3, "V"), ("deg", 12, "PE"),
+    ("mf", 4, "S"), ("red", 2, "V"), ("p", 0, "PE"), ("Q", 7, "V"), ("deg", 13, "PE"),
+    ("deg", 14, "PE"), ("sq", 2, "S"), ("mf", 7, "S"), ("Q", 9, "V"), ("deg", 15, "PE"),
+    ("h", 11, "PE"), ("R", 11, "S"), ("h", 13, "PE"), ("s", 5, "V"), ("h", 14, "PE"),
+    ("rec", 2, "V"), ("s", 7, "V"), ("mg", 1, "V"), ("mf", 9, "S"), ("red", 3, "V"),
+    ("Q", 10, "V"), ("mf", 10, "S"), ("p", 20, "PE"), ("s", 6, "V"), ("sq", 3, "S"),
+    ("p", 28, "PE"), ("mf", 8, "S"), ("h", 15, "PE"), ("s", 4, "V"), ("mf", 11, "S"),
+    ("h", 12, "PE"), ("rec", 3, "V"), ("Q", 11, "V"), ("mf", 15, "S"), ("p", 24, "PE"),
+    ("qm", 1, "V"), ("mf", 14, "S"), ("mg", 2, "V"), ("p", 4, "PE"), ("mf", 12, "S"),
+    ("p", 8, "PE"), ("mf", 13, "S"), ("p", 21, "PE"), ("s", 8, "V"), ("p", 25, "PE"),
+    ("R", 15, "S"), ("p", 9, "PE"), ("qm", 2, "V"), ("p", 17, "PE"), ("p", 12, "PE"),
+    ("mg", 3, "V"), ("p", 13, "PE"), ("p", 6, "PE"), ("p", 16, "PE"), ("p", 26, "PE"),
+    ("s", 13, "V"), ("p", 18, "PE"), ("R", 12, "S"), ("p", 10, "PE"), ("qm", 3, "V"),
+    ("p", 14, "PE"), ("p", 29, "PE"), ("s", 9, "V"), ("p", 5, "PE"), ("p", 22, "PE"),
+    ("s", 11, "V"), ("p", 15, "PE"), ("p", 27, "PE"), ("R", 13, "S"), ("s", 10, "V"),
+    ("p", 11, "PE"), ("p", 2, "PE"), ("s", 12, "V"), ("p", 31, "PE"), ("p", 7, "PE"),
+    ("ep", 3, "V"), ("p", 3, "PE"), ("p", 1, "PE"), ("ep", 2, "V"), ("p", 19, "PE"),
+    ("R", 14, "S"), ("p", 23, "PE"), ("Q", 12, "V"), ("p", 44, "PE"), ("p", 47, "PE"),
+    ("ep", 0, "V"), ("p", 33, "PE"), ("p", 45, "PE"), ("p", 34, "PE"), ("ep", 4, "V"),
+    ("p", 56, "PE"), ("ep", 5, "V"), ("p", 46, "PE"), ("rl", 2, "S"), ("p", 42, "PE"),
+    ("ep", 1, "V"), ("p", 35, "PE"), ("p", 40, "PE"), ("rl", 5, "S"), ("Q", 13, "V"),
+    ("p", 41, "PE"), ("p", 32, "PE"), ("rl", 1, "S"), ("Q", 14, "V"), ("p", 36, "PE"),
+    ("p", 30, "PE"), ("rl", 0, "S"), ("ep", 6, "V"), ("p", 39, "PE"), ("p", 37, "PE"),
+    ("rl", 3, "S"), ("Q", 15, "V"), ("p", 43, "PE"), ("p", 58, "PE"), ("ep", 11, "V"),
+    ("p", 48, "PE"), ("p", 53, "PE"), ("ep", 8, "V"), ("p", 54, "PE"), ("p", 38, "PE"),
+    ("rl", 11, "S"), ("s", 15, "V"), ("p", 49, "PE"), ("p", 52, "PE"), ("rl", 4, "S"),
+    ("ep", 7, "V"), ("p", 55, "PE"), ("p", 51, "PE"), ("rl", 8, "S"), ("ep", 9, "V"),
+    ("p", 59, "PE"), ("p", 50, "PE"), ("rl", 7, "S"), ("ep", 10, "V"), ("p", 57, "PE"),
+    ("p", 61, "PE"), ("rl", 6, "S"), ("ep", 13, "V"), ("p", 63, "PE"), ("p", 62, "PE"),
+    ("rl", 10, "S"), ("s", 14, "V"), ("p", 60, "PE"), ("rl", 9, "S"), ("ep", 12, "V"),
+    ("rl", 13, "S"), ("ep", 14, "V"), ("rl", 12, "S"), ("ep", 15, "V"), ("rl", 14, "S"),
     ("rl", 15, "V"),
 )
 
@@ -132,7 +132,7 @@ def tile_gcnnodeclassifiernetwork_pa_kernel(tc, A, x, W1, b1, out):
         nc.vector.memset(one_f[:], 1.0)
         brow = const.tile([P, FEAT], BF16, name="brow")
         nc.vector.memset(brow[:], 0.0)
-        nc.scalar.dma_start(out=brow[0:1, :], in_=b1.rearrange("(o c) -> o c", o=1))
+        nc.sync.dma_start(out=brow[0:1, :], in_=b1.rearrange("(o c) -> o c", o=1))
         junk = const.tile([P, 1], F32, name="junk")
         nc.scalar.activation(out=junk[:], in_=one_f[:], func=ACT.Sqrt)
         b_bc = const.tile([P, FEAT], F32, name="b_bc")
@@ -180,7 +180,7 @@ def tile_gcnnodeclassifiernetwork_pa_kernel(tc, A, x, W1, b1, out):
         for kind, n, eng in ORDER:
             if kind == "Wr":
                 wg = grab("k", "wg", 1)
-                nc.vector.tensor_copy(out=grouped(wg[:]), in_=planes(tiles["wraw"][:]))
+                copy_on(eng, grouped(wg[:]), planes(tiles["wraw"][:]))
                 drop("wraw")
             elif kind == "Wq":
                 quantise("w", tiles["wg"][:])
@@ -274,9 +274,7 @@ def tile_gcnnodeclassifiernetwork_pa_kernel(tc, A, x, W1, b1, out):
                 drop("hp%d" % n)
             elif kind == "mg":
                 mg = grab("k", "mg%d" % n, 1)
-                nc.vector.tensor_copy(
-                    out=grouped(mg[:]), in_=tiles["mf%d" % n][:].rearrange("p t (c i) -> p c t i", i=4)
-                )
+                copy_on(eng, grouped(mg[:]), tiles["mf%d" % n][:].rearrange("p t (c i) -> p c t i", i=4))
                 drop("mf%d" % n)
             elif kind == "qm":
                 quantise("m%d" % n, tiles["mg%d" % n][:])

@@ -23,54 +23,53 @@ FLOPS = 2 * NODES * FEAT * FEAT + 2 * NODES * NODES * FEAT
 LOADS = (("a", 0), ("a", 1), ("W", 0), ("x", 0), ("a", 2), ("x", 1), ("a", 3), ("x", 2), ("a", 4), ("x", 3), ("a", 5), ("a", 6), ("a", 7), ("a", 8), ("a", 9), ("a", 10), ("a", 11), ("a", 12), ("a", 13), ("a", 14), ("a", 15))
 
 ORDER = (
-    ("R", 0, "V"), ("deg", 1, "PE"), ("R", 1, "S"), ("Q", 0, "V"), ("pbm", 0, "PE"),
-    ("deg", 0, "PE"), ("Wr", 0, "V"), ("tr", 1, "PE"), ("Wq", 0, "V"), ("tr", 0, "PE"),
-    ("Q", 1, "V"), ("xc", 1, "S"), ("deg", 2, "PE"), ("R", 2, "V"), ("xc", 0, "S"),
-    ("tr", 3, "PE"), ("Q", 2, "V"), ("tr", 2, "PE"), ("xq", 0, "V"), ("xc", 3, "S"),
-    ("deg", 3, "PE"), ("R", 3, "V"), ("xc", 2, "S"), ("pbc", 0, "S"), ("tr", 5, "PE"),
-    ("red", 0, "V"), ("xq", 1, "V"), ("tr", 4, "PE"), ("sq", 0, "S"), ("Q", 3, "V"),
-    ("xc", 5, "S"), ("h", 3, "PE"), ("h", 1, "PE"), ("rec", 0, "V"), ("xc", 4, "S"),
-    ("R", 4, "V"), ("mf", 1, "S"), ("tr", 7, "PE"), ("mf", 3, "S"), ("xq", 2, "V"),
-    ("h", 4, "PE"), ("h", 2, "PE"), ("xc", 7, "S"), ("Q", 4, "V"), ("h", 6, "PE"),
-    ("h", 0, "PE"), ("mf", 2, "S"), ("deg", 5, "PE"), ("s", 1, "V"), ("h", 5, "PE"),
-    ("mf", 0, "S"), ("deg", 6, "PE"), ("s", 3, "V"), ("R", 6, "S"), ("R", 5, "V"),
-    ("deg", 7, "PE"), ("deg", 4, "PE"), ("tr", 6, "PE"), ("s", 2, "V"), ("R", 7, "V"),
-    ("deg", 8, "PE"), ("h", 7, "PE"), ("R", 8, "S"), ("h", 8, "PE"), ("Q", 5, "V"),
-    ("Q", 6, "V"), ("red", 1, "V"), ("mg", 0, "V"), ("h", 10, "PE"), ("sq", 1, "S"),
-    ("R", 9, "S"), ("deg", 11, "PE"), ("deg", 10, "PE"), ("s", 0, "V"), ("deg", 9, "PE"),
-    ("qm", 0, "V"), ("rec", 1, "V"), ("Q", 8, "V"), ("xc", 6, "S"), ("R", 10, "V"),
-    ("mf", 5, "S"), ("h", 9, "PE"), ("mf", 6, "S"), ("xq", 3, "V"), ("deg", 12, "PE"),
-    ("mf", 4, "S"), ("red", 2, "V"), ("p", 0, "PE"), ("Q", 7, "V"), ("deg", 13, "PE"),
-    ("deg", 14, "PE"), ("sq", 2, "S"), ("mf", 7, "S"), ("Q", 9, "V"), ("deg", 15, "PE"),
-    ("h", 11, "PE"), ("R", 11, "S"), ("h", 13, "PE"), ("s", 5, "V"), ("h", 14, "PE"),
-    ("rec", 2, "V"), ("s", 7, "V"), ("mg", 1, "V"), ("mf", 9, "S"), ("red", 3, "V"),
-    ("Q", 10, "V"), ("mf", 10, "S"), ("p", 20, "PE"), ("s", 6, "V"), ("sq", 3, "S"),
-    ("p", 28, "PE"), ("mf", 8, "S"), ("h", 15, "PE"), ("s", 4, "V"), ("mf", 11, "S"),
-    ("h", 12, "PE"), ("rec", 3, "V"), ("Q", 11, "V"), ("mf", 15, "S"), ("p", 24, "PE"),
-    ("qm", 1, "V"), ("mf", 14, "S"), ("mg", 2, "V"), ("p", 4, "PE"), ("mf", 12, "S"),
-    ("p", 8, "PE"), ("mf", 13, "S"), ("p", 21, "PE"), ("s", 8, "V"), ("p", 25, "PE"),
-    ("R", 15, "S"), ("p", 9, "PE"), ("qm", 2, "V"), ("p", 17, "PE"), ("p", 12, "PE"),
-    ("mg", 3, "V"), ("p", 13, "PE"), ("p", 6, "PE"), ("p", 16, "PE"), ("p", 26, "PE"),
-    ("s", 13, "V"), ("p", 18, "PE"), ("R", 12, "S"), ("p", 10, "PE"), ("qm", 3, "V"),
-    ("p", 14, "PE"), ("p", 29, "PE"), ("s", 9, "V"), ("p", 5, "PE"), ("p", 22, "PE"),
-    ("s", 11, "V"), ("p", 15, "PE"), ("p", 27, "PE"), ("R", 13, "S"), ("s", 10, "V"),
-    ("p", 11, "PE"), ("p", 2, "PE"), ("s", 12, "V"), ("p", 31, "PE"), ("p", 7, "PE"),
-    ("ep", 3, "V"), ("p", 3, "PE"), ("p", 1, "PE"), ("ep", 2, "V"), ("p", 19, "PE"),
-    ("R", 14, "S"), ("p", 23, "PE"), ("Q", 12, "V"), ("p", 44, "PE"), ("p", 47, "PE"),
-    ("ep", 0, "V"), ("p", 33, "PE"), ("p", 45, "PE"), ("p", 34, "PE"), ("ep", 4, "V"),
-    ("p", 56, "PE"), ("ep", 5, "V"), ("p", 46, "PE"), ("rl", 2, "S"), ("p", 42, "PE"),
-    ("ep", 1, "V"), ("p", 35, "PE"), ("p", 40, "PE"), ("rl", 5, "S"), ("Q", 13, "V"),
-    ("p", 41, "PE"), ("p", 32, "PE"), ("rl", 1, "S"), ("Q", 14, "V"), ("p", 36, "PE"),
-    ("p", 30, "PE"), ("rl", 0, "S"), ("ep", 6, "V"), ("p", 39, "PE"), ("p", 37, "PE"),
-    ("rl", 3, "S"), ("Q", 15, "V"), ("p", 43, "PE"), ("p", 58, "PE"), ("ep", 11, "V"),
-    ("p", 48, "PE"), ("p", 53, "PE"), ("ep", 8, "V"), ("p", 54, "PE"), ("p", 38, "PE"),
-    ("rl", 11, "S"), ("s", 15, "V"), ("p", 49, "PE"), ("p", 52, "PE"), ("rl", 4, "S"),
-    ("ep", 7, "V"), ("p", 55, "PE"), ("p", 51, "PE"), ("rl", 8, "S"), ("ep", 9, "V"),
-    ("p", 59, "PE"), ("p", 50, "PE"), ("rl", 7, "S"), ("ep", 10, "V"), ("p", 57, "PE"),
-    ("p", 61, "PE"), ("rl", 6, "S"), ("ep", 13, "V"), ("p", 63, "PE"), ("p", 62, "PE"),
-    ("rl", 10, "S"), ("s", 14, "V"), ("p", 60, "PE"), ("rl", 9, "S"), ("ep", 12, "V"),
-    ("rl", 13, "S"), ("ep", 14, "V"), ("rl", 12, "S"), ("ep", 15, "V"), ("rl", 14, "S"),
-    ("rl", 15, "V"),
+    ("R", 0, "V"), ("pbm", 0, "PE"), ("R", 1, "S"), ("Q", 0, "V"), ("deg", 1, "PE"),
+    ("deg", 0, "PE"), ("Wr", 0, "V"), ("pbc", 0, "S"), ("tr", 0, "PE"), ("Wq", 0, "V"),
+    ("tr", 1, "PE"), ("Q", 1, "V"), ("xc", 0, "S"), ("deg", 2, "PE"), ("R", 2, "V"),
+    ("xc", 1, "S"), ("tr", 2, "PE"), ("xq", 0, "V"), ("tr", 3, "PE"), ("Q", 2, "V"),
+    ("xc", 2, "S"), ("deg", 3, "PE"), ("R", 3, "V"), ("xc", 3, "S"), ("tr", 4, "PE"),
+    ("red", 0, "V"), ("xq", 1, "V"), ("tr", 5, "PE"), ("sq", 0, "S"), ("Q", 3, "V"),
+    ("xc", 4, "S"), ("h", 3, "PE"), ("h", 1, "PE"), ("R", 4, "V"), ("xc", 5, "S"),
+    ("h", 0, "PE"), ("h", 2, "PE"), ("mf", 1, "S"), ("h", 5, "PE"), ("tr", 6, "PE"),
+    ("xq", 2, "V"), ("mf", 3, "S"), ("h", 6, "PE"), ("Q", 4, "V"), ("mf", 0, "S"),
+    ("h", 7, "PE"), ("tr", 7, "PE"), ("s", 3, "V"), ("mf", 2, "S"), ("h", 8, "PE"),
+    ("R", 5, "V"), ("xc", 6, "S"), ("h", 10, "PE"), ("deg", 6, "PE"), ("deg", 5, "PE"),
+    ("R", 6, "S"), ("h", 4, "PE"), ("mg", 0, "V"), ("deg", 7, "PE"), ("deg", 4, "PE"),
+    ("Q", 5, "V"), ("xc", 7, "S"), ("qm", 0, "V"), ("R", 8, "S"), ("s", 1, "V"),
+    ("deg", 9, "PE"), ("s", 2, "V"), ("s", 0, "V"), ("deg", 10, "PE"), ("deg", 8, "PE"),
+    ("Q", 6, "V"), ("R", 9, "S"), ("deg", 11, "PE"), ("xq", 3, "V"), ("red", 1, "V"),
+    ("R", 7, "V"), ("h", 11, "PE"), ("R", 10, "V"), ("sq", 1, "S"), ("mf", 4, "S"),
+    ("mf", 7, "S"), ("Q", 7, "V"), ("h", 9, "PE"), ("mf", 5, "S"), ("Q", 8, "V"),
+    ("deg", 12, "PE"), ("deg", 13, "PE"), ("mf", 6, "S"), ("Q", 10, "V"), ("h", 13, "PE"),
+    ("deg", 14, "PE"), ("Q", 9, "V"), ("deg", 15, "PE"), ("h", 14, "PE"), ("red", 2, "V"),
+    ("s", 7, "V"), ("p", 24, "PE"), ("sq", 2, "S"), ("s", 4, "V"), ("mf", 11, "S"),
+    ("mg", 1, "V"), ("mf", 8, "S"), ("h", 12, "PE"), ("mf", 10, "S"), ("h", 15, "PE"),
+    ("s", 5, "V"), ("mf", 9, "S"), ("s", 8, "V"), ("R", 11, "S"), ("s", 6, "V"),
+    ("qm", 1, "V"), ("red", 3, "V"), ("mg", 2, "V"), ("p", 1, "PE"), ("sq", 3, "S"),
+    ("p", 9, "PE"), ("mf", 12, "S"), ("p", 12, "PE"), ("p", 0, "PE"), ("Q", 11, "V"),
+    ("mf", 15, "S"), ("p", 13, "PE"), ("p", 21, "PE"), ("qm", 2, "V"), ("mf", 13, "S"),
+    ("p", 25, "PE"), ("p", 29, "PE"), ("s", 9, "V"), ("mf", 14, "S"), ("p", 8, "PE"),
+    ("p", 16, "PE"), ("s", 13, "V"), ("R", 12, "S"), ("p", 30, "PE"), ("p", 22, "PE"),
+    ("mg", 3, "V"), ("p", 26, "PE"), ("p", 20, "PE"), ("p", 18, "PE"), ("p", 6, "PE"),
+    ("s", 12, "V"), ("p", 10, "PE"), ("R", 14, "S"), ("p", 5, "PE"), ("qm", 3, "V"),
+    ("p", 28, "PE"), ("p", 17, "PE"), ("s", 10, "V"), ("p", 2, "PE"), ("p", 19, "PE"),
+    ("s", 11, "V"), ("p", 23, "PE"), ("p", 15, "PE"), ("Q", 12, "V"), ("p", 27, "PE"),
+    ("R", 13, "S"), ("p", 7, "PE"), ("ep", 4, "V"), ("p", 11, "PE"), ("p", 4, "PE"),
+    ("ep", 6, "V"), ("p", 3, "PE"), ("p", 44, "PE"), ("ep", 5, "V"), ("p", 39, "PE"),
+    ("ep", 0, "V"), ("rl", 4, "S"), ("p", 37, "PE"), ("p", 31, "PE"), ("ep", 1, "V"),
+    ("R", 15, "S"), ("p", 14, "PE"), ("p", 43, "PE"), ("Q", 14, "V"), ("p", 36, "PE"),
+    ("p", 33, "PE"), ("Q", 13, "V"), ("p", 38, "PE"), ("p", 48, "PE"), ("ep", 7, "V"),
+    ("p", 32, "PE"), ("p", 50, "PE"), ("rl", 0, "S"), ("ep", 9, "V"), ("p", 45, "PE"),
+    ("p", 34, "PE"), ("rl", 1, "S"), ("s", 14, "V"), ("p", 47, "PE"), ("p", 52, "PE"),
+    ("rl", 7, "S"), ("ep", 2, "V"), ("p", 56, "PE"), ("p", 35, "PE"), ("rl", 6, "S"),
+    ("ep", 3, "V"), ("p", 57, "PE"), ("p", 40, "PE"), ("rl", 2, "S"), ("Q", 15, "V"),
+    ("p", 42, "PE"), ("p", 41, "PE"), ("rl", 5, "S"), ("ep", 8, "V"), ("p", 46, "PE"),
+    ("p", 53, "PE"), ("rl", 9, "S"), ("s", 15, "V"), ("p", 63, "PE"), ("p", 51, "PE"),
+    ("rl", 3, "S"), ("ep", 10, "V"), ("p", 58, "PE"), ("p", 49, "PE"), ("rl", 8, "S"),
+    ("ep", 11, "V"), ("p", 55, "PE"), ("p", 54, "PE"), ("rl", 10, "S"), ("ep", 12, "V"),
+    ("p", 60, "PE"), ("p", 59, "PE"), ("rl", 11, "S"), ("ep", 13, "V"), ("p", 61, "PE"),
+    ("p", 62, "PE"), ("rl", 12, "S"), ("ep", 14, "V"), ("rl", 13, "S"), ("ep", 15, "V"),
+    ("rl", 14, "S"), ("rl", 15, "V"),
 )
 
 
@@ -126,15 +125,14 @@ def tile_gcnnodeclassifiernetwork_pa_kernel(tc, A, x, W1, b1, out):
 
         ident = const.tile([P, P], F32, name="ident")
         make_identity(nc, ident[:])
-        ones_bf = const.tile([P, P], BF16, name="ones_bf")
-        nc.vector.memset(ones_bf[:], 1.0)
-        one_f = const.tile([P, 1], F32, name="one_f")
-        nc.vector.memset(one_f[:], 1.0)
         brow = const.tile([P, FEAT], BF16, name="brow")
         nc.vector.memset(brow[:], 0.0)
-        nc.sync.dma_start(out=brow[0:1, :], in_=b1.rearrange("(o c) -> o c", o=1))
+        one_f = const.tile([P, 1], F32, name="one_f")
+        nc.vector.memset(one_f[:], 1.0)
+        ones_bf = const.tile([P, P], BF16, name="ones_bf")
+        nc.vector.memset(ones_bf[:], 1.0)
         junk = const.tile([P, 1], F32, name="junk")
-        nc.scalar.activation(out=junk[:], in_=one_f[:], func=ACT.Sqrt)
+        nc.scalar.activation(out=junk[:], in_=one_f[:], func=ACT.Abs_reciprocal_sqrt)
         b_bc = const.tile([P, FEAT], F32, name="b_bc")
 
         x_view = x.rearrange("(T p) k -> p T k", p=P)
@@ -143,7 +141,9 @@ def tile_gcnnodeclassifiernetwork_pa_kernel(tc, A, x, W1, b1, out):
         grab("k", "wraw", 1)
         for q in range(4):
             grab("k", "xraw%d" % q, 2)
-        for what, n in LOADS:
+        for k, (what, n) in enumerate(LOADS):
+            if k == 2:
+                nc.sync.dma_start(out=brow[0:1, :], in_=b1.rearrange("(o c) -> o c", o=1))
             if what == "W":
                 nc.sync.dma_start(
                     out=tiles["wraw"][:].rearrange("q (u r) -> q u r", u=2),
@@ -240,11 +240,15 @@ def tile_gcnnodeclassifiernetwork_pa_kernel(tc, A, x, W1, b1, out):
                 small["deg%d" % n] = deg
                 drop("dg%d" % n)
             elif kind == "sq":
-                rd = const.tile([P, 4], F32, name="rd%d" % n)
+                d = const.tile([P, 4], F32, name="d%d" % n)
                 nc.scalar.activation(
-                    out=rd[:], in_=small["deg%d" % n][:], func=ACT.Sqrt, bias=one_f[:, 0:1], scale=1.0
+                    out=d[:],
+                    in_=small["deg%d" % n][:],
+                    func=ACT.Abs_reciprocal_sqrt,
+                    bias=one_f[:, 0:1],
+                    scale=1.0,
                 )
-                small["rd%d" % n] = rd
+                small["d%d" % n] = d
             elif kind == "rec":
                 d = const.tile([P, 4], F32, name="d%d" % n)
                 nc.vector.reciprocal(out=d[:], in_=small["rd%d" % n][:])

@@ -13,64 +13,18 @@ ALU = mybir.AluOpType
 AXIS = mybir.AxisListType
 
 P = 128
+PACK = 4
 NODES = 2048
 FEAT = 512
-UNIT = 2048
-K_SLOTS = 9
+BLOCKS = NODES // (P * PACK)
+TILES = NODES // P
+UNIT = PACK * FEAT
+
+VECTOR_UNITS = (0, 2, 3, 4, 5, 7)
+GROUPED_SLOTS = 6
+RELU_ON_VECTOR_FROM = TILES - 2
 
 FLOPS = 2 * NODES * FEAT * FEAT + 2 * NODES * NODES * FEAT
-
-LOADS = (("a", 0), ("a", 1), ("W", 0), ("x", 0), ("a", 2), ("x", 1), ("a", 3), ("x", 2), ("a", 4), ("x", 3), ("a", 5), ("a", 6), ("a", 7), ("a", 8), ("a", 9), ("a", 10), ("a", 11), ("a", 12), ("a", 13), ("a", 14), ("a", 15))
-
-ORDER = (
-    ("R", 0, "V"), ("pbm", 0, "PE"), ("R", 1, "S"), ("Q", 0, "V"), ("deg", 1, "PE"),
-    ("deg", 0, "PE"), ("Wr", 0, "V"), ("pbc", 0, "S"), ("tr", 0, "PE"), ("Wq", 0, "V"),
-    ("tr", 1, "PE"), ("Q", 1, "V"), ("xc", 0, "S"), ("deg", 2, "PE"), ("R", 2, "V"),
-    ("xc", 1, "S"), ("tr", 2, "PE"), ("xq", 0, "V"), ("tr", 3, "PE"), ("Q", 2, "V"),
-    ("xc", 2, "S"), ("deg", 3, "PE"), ("R", 3, "V"), ("xc", 3, "S"), ("tr", 4, "PE"),
-    ("red", 0, "V"), ("xq", 1, "V"), ("tr", 5, "PE"), ("sq", 0, "S"), ("Q", 3, "V"),
-    ("xc", 4, "S"), ("h", 3, "PE"), ("h", 1, "PE"), ("R", 4, "V"), ("xc", 5, "S"),
-    ("h", 0, "PE"), ("h", 2, "PE"), ("mf", 1, "S"), ("h", 5, "PE"), ("tr", 6, "PE"),
-    ("xq", 2, "V"), ("mf", 3, "S"), ("h", 6, "PE"), ("Q", 4, "V"), ("mf", 0, "S"),
-    ("h", 7, "PE"), ("tr", 7, "PE"), ("s", 3, "V"), ("mf", 2, "S"), ("h", 8, "PE"),
-    ("R", 5, "V"), ("xc", 6, "S"), ("h", 10, "PE"), ("deg", 6, "PE"), ("deg", 5, "PE"),
-    ("R", 6, "S"), ("h", 4, "PE"), ("mg", 0, "V"), ("deg", 7, "PE"), ("deg", 4, "PE"),
-    ("Q", 5, "V"), ("xc", 7, "S"), ("qm", 0, "V"), ("R", 8, "S"), ("s", 1, "V"),
-    ("deg", 9, "PE"), ("s", 2, "V"), ("s", 0, "V"), ("deg", 10, "PE"), ("deg", 8, "PE"),
-    ("Q", 6, "V"), ("R", 9, "S"), ("deg", 11, "PE"), ("xq", 3, "V"), ("red", 1, "V"),
-    ("R", 7, "V"), ("h", 11, "PE"), ("R", 10, "V"), ("sq", 1, "S"), ("mf", 4, "S"),
-    ("mf", 7, "S"), ("Q", 7, "V"), ("h", 9, "PE"), ("mf", 5, "S"), ("Q", 8, "V"),
-    ("deg", 12, "PE"), ("deg", 13, "PE"), ("mf", 6, "S"), ("Q", 10, "V"), ("h", 13, "PE"),
-    ("deg", 14, "PE"), ("Q", 9, "V"), ("deg", 15, "PE"), ("h", 14, "PE"), ("red", 2, "V"),
-    ("s", 7, "V"), ("p", 24, "PE"), ("sq", 2, "S"), ("s", 4, "V"), ("mf", 11, "S"),
-    ("mg", 1, "V"), ("mf", 8, "S"), ("h", 12, "PE"), ("mf", 10, "S"), ("h", 15, "PE"),
-    ("s", 5, "V"), ("mf", 9, "S"), ("s", 8, "V"), ("R", 11, "S"), ("s", 6, "V"),
-    ("qm", 1, "V"), ("red", 3, "V"), ("mg", 2, "V"), ("p", 1, "PE"), ("sq", 3, "S"),
-    ("p", 9, "PE"), ("mf", 12, "S"), ("p", 12, "PE"), ("p", 0, "PE"), ("Q", 11, "V"),
-    ("mf", 15, "S"), ("p", 13, "PE"), ("p", 21, "PE"), ("qm", 2, "V"), ("mf", 13, "S"),
-    ("p", 25, "PE"), ("p", 29, "PE"), ("s", 9, "V"), ("mf", 14, "S"), ("p", 8, "PE"),
-    ("p", 16, "PE"), ("s", 13, "V"), ("R", 12, "S"), ("p", 30, "PE"), ("p", 22, "PE"),
-    ("mg", 3, "V"), ("p", 26, "PE"), ("p", 20, "PE"), ("p", 18, "PE"), ("p", 6, "PE"),
-    ("s", 12, "V"), ("p", 10, "PE"), ("R", 14, "S"), ("p", 5, "PE"), ("qm", 3, "V"),
-    ("p", 28, "PE"), ("p", 17, "PE"), ("s", 10, "V"), ("p", 2, "PE"), ("p", 19, "PE"),
-    ("s", 11, "V"), ("p", 23, "PE"), ("p", 15, "PE"), ("Q", 12, "V"), ("p", 27, "PE"),
-    ("R", 13, "S"), ("p", 7, "PE"), ("ep", 4, "V"), ("p", 11, "PE"), ("p", 4, "PE"),
-    ("ep", 6, "V"), ("p", 3, "PE"), ("p", 44, "PE"), ("ep", 5, "V"), ("p", 39, "PE"),
-    ("ep", 0, "V"), ("rl", 4, "S"), ("p", 37, "PE"), ("p", 31, "PE"), ("ep", 1, "V"),
-    ("R", 15, "S"), ("p", 14, "PE"), ("p", 43, "PE"), ("Q", 14, "V"), ("p", 36, "PE"),
-    ("p", 33, "PE"), ("Q", 13, "V"), ("p", 38, "PE"), ("p", 48, "PE"), ("ep", 7, "V"),
-    ("p", 32, "PE"), ("p", 50, "PE"), ("rl", 0, "S"), ("ep", 9, "V"), ("p", 45, "PE"),
-    ("p", 34, "PE"), ("rl", 1, "S"), ("s", 14, "V"), ("p", 47, "PE"), ("p", 52, "PE"),
-    ("rl", 7, "S"), ("ep", 2, "V"), ("p", 56, "PE"), ("p", 35, "PE"), ("rl", 6, "S"),
-    ("ep", 3, "V"), ("p", 57, "PE"), ("p", 40, "PE"), ("rl", 2, "S"), ("Q", 15, "V"),
-    ("p", 42, "PE"), ("p", 41, "PE"), ("rl", 5, "S"), ("ep", 8, "V"), ("p", 46, "PE"),
-    ("p", 53, "PE"), ("rl", 9, "S"), ("s", 15, "V"), ("p", 63, "PE"), ("p", 51, "PE"),
-    ("rl", 3, "S"), ("ep", 10, "V"), ("p", 58, "PE"), ("p", 49, "PE"), ("rl", 8, "S"),
-    ("ep", 11, "V"), ("p", 55, "PE"), ("p", 54, "PE"), ("rl", 10, "S"), ("ep", 12, "V"),
-    ("p", 60, "PE"), ("p", 59, "PE"), ("rl", 11, "S"), ("ep", 13, "V"), ("p", 61, "PE"),
-    ("p", 62, "PE"), ("rl", 12, "S"), ("ep", 14, "V"), ("rl", 13, "S"), ("ep", 15, "V"),
-    ("rl", 14, "S"), ("rl", 15, "V"),
-)
 
 
 def tile_gcnnodeclassifiernetwork_pa_kernel(tc, A, x, W1, b1, out):
@@ -78,262 +32,313 @@ def tile_gcnnodeclassifiernetwork_pa_kernel(tc, A, x, W1, b1, out):
     with ExitStack() as ctx:
         ctx.enter_context(tc.manual_schedule())
         const = ctx.enter_context(tc.tile_pool(name="const", bufs=1))
-        keep = ctx.enter_context(tc.tile_pool(name="keep", bufs=1))
         raw = ctx.enter_context(tc.tile_pool(name="raw", bufs=1))
-        kpool = ctx.enter_context(tc.tile_pool(name="kpool", bufs=1))
-        mpool = ctx.enter_context(tc.tile_pool(name="mpool", bufs=1))
+        keep = ctx.enter_context(tc.tile_pool(name="keep", bufs=1))
+        stage = ctx.enter_context(tc.tile_pool(name="stage", bufs=1))
         psum = ctx.enter_context(tc.psum_pool(name="psum", bufs=1))
 
-        free = {"b": list(range(8)), "k": list(range(K_SLOTS)), "m": [0, 1]}
-        tiles = {}
-        slot_of = {}
-        readers = {}
+        def bank(index, name):
+            return psum.tile([P, FEAT], F32, tag="bank%d" % index, name=name)
 
-        def grab(pool, name, n_readers):
-            if name in tiles:
-                return tiles[name]
-            assert free[pool], name
-            idx = free[pool].pop(0)
-            slot_of[name] = (pool, idx)
-            readers[name] = n_readers
-            if pool == "b":
-                t = psum.tile([P, FEAT], F32, tag="b%d" % idx, name=name)
-            elif pool == "k":
-                t = kpool.tile([P, UNIT], BF16, tag="k%d" % idx, name=name, align_bytes=64)
+        grouped_made = []
+
+        def new_grouped(name):
+            slot = len(grouped_made) % GROUPED_SLOTS
+            grouped_made.append(name)
+            return stage.tile([P, UNIT], BF16, tag="grouped%d" % slot, name=name, align_bytes=64)
+
+        def by_plane(tile_ap):
+            return tile_ap.rearrange("p (t c i) -> p c t i", t=PACK, i=4)
+
+        def by_word(tile_ap):
+            return tile_ap.rearrange("p (c i t) -> p c t i", i=4, t=PACK)
+
+        def quantise(name, grouped):
+            codes = keep.tile([P, FEAT], U32, name=name + "_codes", align_bytes=64)
+            scales = keep.tile([P, FEAT], U8, name=name + "_scales", align_bytes=64)
+            nc.vector.quantize_mx(out=codes[:].bitcast(FP8X4), scales=scales[:], in_=grouped[:])
+            return codes, scales
+
+        b_row = const.tile([P, FEAT], BF16, name="b_row")
+        nc.vector.memset(b_row[:], 0.0)
+        one = const.tile([P, 1], F32, name="one")
+        nc.vector.memset(one[:], 1.0)
+        ones = const.tile([P, P], BF16, name="ones")
+        nc.vector.memset(ones[:], 1.0)
+        identity = const.tile([P, P], F32, name="identity")
+        make_identity(nc, identity[:])
+        warm = const.tile([P, 1], F32, name="warm")
+        nc.scalar.activation(out=warm[:], in_=one[:], func=ACT.Abs_reciprocal_sqrt)
+
+        a_rows = A.rearrange("(g t p) j -> g p t j", t=PACK, p=P)
+        x_rows = x.rearrange("(T p) k -> p T k", p=P)
+        a_raw = {}
+        x_raw = {}
+
+        def load_unit(u):
+            b, g = divmod(u, BLOCKS)
+            a_raw[u] = raw.tile([P, UNIT], BF16, name="a_raw%d" % u)
+            nc.sync.dma_start(
+                out=a_raw[u][:].rearrange("p (t j) -> p t j", t=PACK),
+                in_=a_rows[g, :, :, FEAT * b : FEAT * (b + 1)],
+            )
+
+        def load_x(q):
+            x_raw[q] = raw.tile([P, UNIT], BF16, name="x_raw%d" % q)
+            nc.sync.dma_start(
+                out=x_raw[q][:].rearrange("p (T k) -> p T k", T=PACK),
+                in_=x_rows[:, PACK * q : PACK * (q + 1), :],
+            )
+
+        load_unit(0)
+        load_unit(1)
+        nc.sync.dma_start(out=b_row[0:1, :], in_=b1.rearrange("(o c) -> o c", o=1))
+        w_raw = raw.tile([P, UNIT], BF16, name="w_raw")
+        nc.sync.dma_start(
+            out=w_raw[:].rearrange("q (u r) -> q u r", u=2),
+            in_=W1.rearrange("(u q e) c -> q u (e c)", u=2, q=P, e=2),
+        )
+        for q in range(BLOCKS):
+            load_x(q)
+            load_unit(q + 2)
+        for u in range(BLOCKS + 2, BLOCKS * BLOCKS):
+            load_unit(u)
+
+        sums = {}
+        a_grouped = {}
+        a_mx = {}
+
+        def column_sums(u):
+            b, g = divmod(u, BLOCKS)
+            if g == 0:
+                sums[b] = bank(6 + b % 2, "sums%d" % b)
+            for jl in range(BLOCKS):
+                for t in range(PACK):
+                    col = 16 * jl + PACK * g + t
+                    src = FEAT * t + P * jl
+                    nc.tensor.matmul(
+                        out=sums[b][:, col : col + 1],
+                        lhsT=a_raw[u][:, src : src + P],
+                        rhs=ones[:, 0:1],
+                        start=True,
+                        stop=True,
+                    )
+
+        def regroup(u):
+            a_grouped[u] = new_grouped("a_grouped%d" % u)
+            if u in VECTOR_UNITS:
+                nc.vector.tensor_copy(out=by_word(a_grouped[u][:]), in_=by_plane(a_raw[u][:]))
             else:
-                t = mpool.tile([P, 4, FEAT], F32, tag="m%d" % idx, name=name)
-            tiles[name] = t
-            return t
+                nc.scalar.copy(out=by_word(a_grouped[u][:]), in_=by_plane(a_raw[u][:]))
 
-        def drop(name):
-            readers[name] -= 1
-            if readers[name] == 0:
-                pool, idx = slot_of[name]
-                free[pool].append(idx)
+        def quantise_unit(u):
+            a_mx[u] = quantise("a%d" % u, a_grouped[u])
 
-        def grouped(tile_ap):
-            return tile_ap.rearrange("p (c i t) -> p c t i", i=4, t=4)
+        x_t = {}
+        x_grouped = {}
+        x_mx = {}
 
-        def planes(tile_ap):
-            return tile_ap.rearrange("p (t c i) -> p c t i", t=4, i=4)
-
-        def copy_on(eng, dst, src):
-            if eng == "V":
-                nc.vector.tensor_copy(out=dst, in_=src)
-            else:
-                nc.scalar.copy(out=dst, in_=src)
-
-        ident = const.tile([P, P], F32, name="ident")
-        make_identity(nc, ident[:])
-        brow = const.tile([P, FEAT], BF16, name="brow")
-        nc.vector.memset(brow[:], 0.0)
-        one_f = const.tile([P, 1], F32, name="one_f")
-        nc.vector.memset(one_f[:], 1.0)
-        ones_bf = const.tile([P, P], BF16, name="ones_bf")
-        nc.vector.memset(ones_bf[:], 1.0)
-        junk = const.tile([P, 1], F32, name="junk")
-        nc.scalar.activation(out=junk[:], in_=one_f[:], func=ACT.Abs_reciprocal_sqrt)
-        b_bc = const.tile([P, FEAT], F32, name="b_bc")
-
-        x_view = x.rearrange("(T p) k -> p T k", p=P)
-        a_view = A.rearrange("(g t p) j -> g p t j", t=4, p=P)
-        araw = {}
-        grab("k", "wraw", 1)
-        for q in range(4):
-            grab("k", "xraw%d" % q, 2)
-        for k, (what, n) in enumerate(LOADS):
-            if k == 2:
-                nc.sync.dma_start(out=brow[0:1, :], in_=b1.rearrange("(o c) -> o c", o=1))
-            if what == "W":
-                nc.sync.dma_start(
-                    out=tiles["wraw"][:].rearrange("q (u r) -> q u r", u=2),
-                    in_=W1.rearrange("(u q e) c -> q u (e c)", u=2, q=P, e=2),
-                )
-            elif what == "x":
-                nc.sync.dma_start(
-                    out=tiles["xraw%d" % n][:].rearrange("p (T k) -> p T k", T=4),
-                    in_=x_view[:, 4 * n : 4 * n + 4, :],
-                )
-            else:
-                b, g = divmod(n, 4)
-                ar = raw.tile([P, UNIT], BF16, name="araw%d" % n)
-                nc.sync.dma_start(
-                    out=ar[:].rearrange("p (t j) -> p t j", t=4),
-                    in_=a_view[g, :, :, FEAT * b : FEAT * b + FEAT],
-                )
-                araw[n] = ar
-
-        codes = {}
-        scales = {}
-
-        def quantise(name, src):
-            cq = keep.tile([P, FEAT], U32, name="c_" + name, align_bytes=64)
-            sq = keep.tile([P, FEAT], U8, name="s_" + name, align_bytes=64)
-            nc.vector.quantize_mx(out=cq[:].bitcast(FP8X4), scales=sq[:], in_=src)
-            codes[name] = cq
-            scales[name] = sq
-
-        small = {}
-        s_tiles = {}
-        n_pass = {}
-
-        for kind, n, eng in ORDER:
-            if kind == "Wr":
-                wg = grab("k", "wg", 1)
-                copy_on(eng, grouped(wg[:]), planes(tiles["wraw"][:]))
-                drop("wraw")
-            elif kind == "Wq":
-                quantise("w", tiles["wg"][:])
-                drop("wg")
-            elif kind == "pbm":
-                pb = grab("b", "pb", 1)
-                nc.tensor.matmul(out=pb[:], lhsT=ones_bf[:], rhs=brow[:], start=True, stop=True)
-            elif kind == "pbc":
-                copy_on(eng, b_bc[:], tiles["pb"][:])
-                drop("pb")
-            elif kind == "tr":
-                q, hh = divmod(n, 2)
-                tp = grab("b", "tp%d" % n, 1)
-                xw = tiles["xraw%d" % q][:].bitcast(F32)
+        def transpose_x(q):
+            words = x_raw[q][:].bitcast(F32)
+            for half in range(2):
+                x_t[(q, half)] = bank(4 + half, "x_t%d_%d" % (q, half))
                 for tl in range(2):
                     for u in range(2):
-                        col = 256 * (2 * hh + tl) + P * u
+                        src = 256 * (2 * half + tl) + P * u
                         dst = P * (2 * tl + u)
                         nc.tensor.transpose(
-                            out=tp[:, dst : dst + P], in_=xw[:, col : col + P], identity=ident[:]
+                            out=x_t[(q, half)][:, dst : dst + P],
+                            in_=words[:, src : src + P],
+                            identity=identity[:],
                         )
-                drop("xraw%d" % q)
-            elif kind == "xc":
-                q, hh = divmod(n, 2)
-                xg = grab("k", "xg%d" % q, 1)
-                dstv = xg[:].bitcast(F32)[:, 512 * hh : 512 * hh + 512].rearrange(
-                    "p (T r u) -> p T r u", T=2, u=2
+
+        def copy_x(q):
+            x_grouped[q] = new_grouped("x_grouped%d" % q)
+            words = x_grouped[q][:].bitcast(F32)
+            for half in range(2):
+                nc.scalar.copy(
+                    out=words[:, FEAT * half : FEAT * (half + 1)].rearrange(
+                        "p (T r u) -> p T r u", T=2, u=2
+                    ),
+                    in_=x_t[(q, half)][:].rearrange("p (T u r) -> p T r u", T=2, u=2),
                 )
-                srcv = tiles["tp%d" % n][:].rearrange("p (T u r) -> p T r u", T=2, u=2)
-                copy_on(eng, dstv, srcv)
-                drop("tp%d" % n)
-            elif kind == "xq":
-                quantise("x%d" % n, tiles["xg%d" % n][:])
-                drop("xg%d" % n)
-            elif kind == "deg":
-                b, g = divmod(n, 4)
-                dg = grab("b", "dg%d" % b, 1)
-                for jl in range(4):
-                    for t in range(4):
-                        col = 16 * jl + 4 * g + t
-                        src = FEAT * t + P * jl
-                        nc.tensor.matmul(
-                            out=dg[:, col : col + 1],
-                            lhsT=araw[n][:, src : src + P],
-                            rhs=ones_bf[:, 0:1],
-                            start=True,
-                            stop=True,
-                        )
-            elif kind == "red":
-                deg = const.tile([P, 4], F32, name="deg%d" % n)
-                nc.vector.tensor_reduce(
-                    out=deg[:],
-                    in_=tiles["dg%d" % n][:, 0:64].rearrange("p (j r) -> p j r", r=16),
-                    axis=AXIS.X,
-                    op=ALU.add,
-                )
-                small["deg%d" % n] = deg
-                drop("dg%d" % n)
-            elif kind == "sq":
-                d = const.tile([P, 4], F32, name="d%d" % n)
-                nc.scalar.activation(
-                    out=d[:],
-                    in_=small["deg%d" % n][:],
-                    func=ACT.Abs_reciprocal_sqrt,
-                    bias=one_f[:, 0:1],
-                    scale=1.0,
-                )
-                small["d%d" % n] = d
-            elif kind == "rec":
-                d = const.tile([P, 4], F32, name="d%d" % n)
-                nc.vector.reciprocal(out=d[:], in_=small["rd%d" % n][:])
-                small["d%d" % n] = d
-            elif kind == "h":
-                b, t = divmod(n, 4)
-                hp = grab("b", "hp%d" % n, 1)
-                nc.tensor.matmul_mx(
-                    out=hp[:],
-                    lhsT=codes["x%d" % b][:, P * t : P * t + P].bitcast(FP8X4),
-                    lhsT_scale=scales["x%d" % b][:, P * t : P * t + P],
-                    rhs=codes["w"][:].bitcast(FP8X4),
-                    rhs_scale=scales["w"][:],
-                    start=True,
-                    stop=True,
-                )
-            elif kind == "mf":
-                b, t = divmod(n, 4)
-                mf = grab("m", "mf%d" % b, 5)
-                dcol = small["d%d" % b][:, t : t + 1]
-                if eng == "S":
-                    nc.scalar.activation(
-                        out=mf[:, t, :], in_=tiles["hp%d" % n][:], func=ACT.Copy, scale=dcol
-                    )
-                else:
-                    nc.vector.tensor_scalar_mul(out=mf[:, t, :], in0=tiles["hp%d" % n][:], scalar1=dcol)
-                drop("hp%d" % n)
-            elif kind == "mg":
-                mg = grab("k", "mg%d" % n, 1)
-                copy_on(eng, grouped(mg[:]), tiles["mf%d" % n][:].rearrange("p t (c i) -> p c t i", i=4))
-                drop("mf%d" % n)
-            elif kind == "qm":
-                quantise("m%d" % n, tiles["mg%d" % n][:])
-                drop("mg%d" % n)
-            elif kind == "s":
-                b, t = divmod(n, 4)
-                st = keep.tile([P, FEAT], F32, name="s%d" % n)
-                nc.vector.scalar_tensor_tensor(
-                    out=st[:],
-                    in0=tiles["mf%d" % b][:, t, :],
-                    scalar=small["d%d" % b][:, t : t + 1],
-                    in1=b_bc[:],
-                    op0=ALU.mult,
-                    op1=ALU.add,
-                )
-                s_tiles[n] = st
-                drop("mf%d" % b)
-            elif kind == "R":
-                ag = grab("k", "ag%d" % n, 1)
-                copy_on(eng, grouped(ag[:]), planes(araw[n][:]))
-            elif kind == "Q":
-                quantise("a%d" % n, tiles["ag%d" % n][:])
-                drop("ag%d" % n)
-            elif kind == "p":
-                jt, c = divmod(n, 4)
-                acc = grab("b", "acc%d" % jt, 1)
-                k = n_pass.get(jt, 0)
-                n_pass[jt] = k + 1
-                name = "a%d" % (4 * (jt // 4) + c)
-                col = P * (jt % 4)
-                nc.tensor.matmul_mx(
-                    out=acc[:],
-                    lhsT=codes[name][:, col : col + P].bitcast(FP8X4),
-                    lhsT_scale=scales[name][:, col : col + P],
-                    rhs=codes["m%d" % c][:].bitcast(FP8X4),
-                    rhs_scale=scales["m%d" % c][:],
-                    start=(k == 0),
-                    stop=(k == 3),
-                )
-            elif kind == "ep":
-                st = s_tiles[n]
-                nc.vector.scalar_tensor_tensor(
-                    out=st[:],
-                    in0=tiles["acc%d" % n][:],
-                    scalar=small["d%d" % (n // 4)][:, n % 4 : n % 4 + 1],
-                    in1=st[:],
-                    op0=ALU.mult,
-                    op1=ALU.add,
-                )
-                drop("acc%d" % n)
+
+        def quantise_x(q):
+            x_mx[q] = quantise("x%d" % q, x_grouped[q])
+
+        d = {}
+        h = {}
+        m_f32 = {}
+        m_mx = {}
+        self_term = {}
+
+        def inv_sqrt_degree(b):
+            deg = const.tile([P, BLOCKS], F32, name="deg%d" % b)
+            nc.vector.tensor_reduce(
+                out=deg[:],
+                in_=sums[b][:, 0:64].rearrange("p (j r) -> p j r", r=16),
+                axis=AXIS.X,
+                op=ALU.add,
+            )
+            d[b] = const.tile([P, BLOCKS], F32, name="d%d" % b)
+            nc.scalar.activation(
+                out=d[b][:], in_=deg[:], func=ACT.Abs_reciprocal_sqrt, bias=one[:, 0:1], scale=1.0
+            )
+
+        def d_of(T):
+            return d[T // BLOCKS][:, T % BLOCKS : T % BLOCKS + 1]
+
+        def h_pass(T):
+            q, r = divmod(T, PACK)
+            h[T] = bank(T % 4, "h%d" % T)
+            nc.tensor.matmul_mx(
+                out=h[T][:],
+                lhsT=x_mx[q][0][:, P * r : P * (r + 1)].bitcast(FP8X4),
+                lhsT_scale=x_mx[q][1][:, P * r : P * (r + 1)],
+                rhs=w_mx[0][:].bitcast(FP8X4),
+                rhs_scale=w_mx[1][:],
+                start=True,
+                stop=True,
+            )
+
+        def scale_rows(T):
+            g, t = divmod(T, PACK)
+            if t == 0:
+                m_f32[g] = stage.tile([P, PACK, FEAT], F32, tag="m_f32_%d" % (g % 2), name="m_f32_%d" % g)
+            nc.scalar.activation(out=m_f32[g][:, t, :], in_=h[T][:], func=ACT.Copy, scale=d_of(T))
+
+        def self_loop(T):
+            g, t = divmod(T, PACK)
+            self_term[T] = keep.tile([P, FEAT], F32, name="self_term%d" % T)
+            nc.vector.scalar_tensor_tensor(
+                out=self_term[T][:],
+                in0=m_f32[g][:, t, :],
+                scalar=d_of(T),
+                in1=b_all[:],
+                op0=ALU.mult,
+                op1=ALU.add,
+            )
+
+        def pack_m(g):
+            grouped = new_grouped("m_grouped%d" % g)
+            nc.vector.tensor_copy(
+                out=by_word(grouped[:]), in_=m_f32[g][:].rearrange("p t (c i) -> p c t i", i=4)
+            )
+            m_mx[g] = quantise("m%d" % g, grouped)
+
+        acc = {}
+
+        def agg_pass(jt, g):
+            b, jl = divmod(jt, BLOCKS)
+            if g == 0:
+                acc[jt] = bank((jt + 4) % 8, "acc%d" % jt)
+            codes, scales = a_mx[BLOCKS * b + g]
+            nc.tensor.matmul_mx(
+                out=acc[jt][:],
+                lhsT=codes[:, P * jl : P * (jl + 1)].bitcast(FP8X4),
+                lhsT_scale=scales[:, P * jl : P * (jl + 1)],
+                rhs=m_mx[g][0][:].bitcast(FP8X4),
+                rhs_scale=m_mx[g][1][:],
+                start=(g == 0),
+                stop=(g == BLOCKS - 1),
+            )
+
+        def finish(jt):
+            res = self_term[jt]
+            nc.vector.scalar_tensor_tensor(
+                out=res[:], in0=acc[jt][:], scalar=d_of(jt), in1=res[:], op0=ALU.mult, op1=ALU.add
+            )
+            if jt >= RELU_ON_VECTOR_FROM:
+                nc.vector.tensor_scalar_max(out=res[:], in0=res[:], scalar1=0.0)
             else:
-                assert kind == "rl"
-                st = s_tiles[n]
-                if eng == "S":
-                    nc.scalar.activation(out=st[:], in_=st[:], func=ACT.Relu)
-                else:
-                    nc.vector.tensor_scalar_max(out=st[:], in0=st[:], scalar1=0.0)
-                nc.sync.dma_start(out=out[P * n : P * n + P, :], in_=st[:])
+                nc.scalar.activation(out=res[:], in_=res[:], func=ACT.Relu)
+            nc.sync.dma_start(out=out[P * jt : P * (jt + 1), :], in_=res[:])
+
+
+        column_sums(0)
+        regroup(0)
+        quantise_unit(0)
+        column_sums(1)
+        regroup(1)
+        w_grouped = new_grouped("w_grouped")
+        nc.vector.tensor_copy(out=by_word(w_grouped[:]), in_=by_plane(w_raw[:]))
+        w_mx = quantise("w", w_grouped)
+        b_psum = bank(7, "b_psum")
+        nc.tensor.matmul(out=b_psum[:], lhsT=ones[:], rhs=b_row[:], start=True, stop=True)
+        b_all = const.tile([P, FEAT], F32, name="b_all")
+        nc.scalar.copy(out=b_all[:], in_=b_psum[:])
+        transpose_x(0)
+        copy_x(0)
+        quantise_unit(1)
+        column_sums(2)
+        regroup(2)
+        quantise_x(0)
+        quantise_unit(2)
+        transpose_x(1)
+        copy_x(1)
+        column_sums(3)
+        regroup(3)
+
+        inv_sqrt_degree(0)
+        for T in range(PACK):
+            h_pass(T)
+        quantise_x(1)
+        quantise_unit(3)
+        transpose_x(2)
+        copy_x(2)
+        for T in range(PACK):
+            scale_rows(T)
+        column_sums(4)
+        regroup(4)
+        quantise_unit(4)
+        quantise_x(2)
+        transpose_x(3)
+        copy_x(3)
+        column_sums(5)
+        regroup(5)
+        quantise_unit(5)
+        pack_m(0)
+        quantise_x(3)
+        column_sums(6)
+        regroup(6)
+        column_sums(7)
+
+        for b in range(1, BLOCKS):
+            for T in range(PACK * b, PACK * (b + 1)):
+                h_pass(T)
+            if b + 1 < BLOCKS:
+                for u in range(BLOCKS * (b + 1), BLOCKS * (b + 2)):
+                    column_sums(u)
+            inv_sqrt_degree(b)
+            for T in range(PACK * b, PACK * (b + 1)):
+                scale_rows(T)
+            for T in range(PACK * (b - 1), PACK * b):
+                self_loop(T)
+            if b == 1:
+                regroup(7)
+            quantise_unit(2 * b + 4)
+            quantise_unit(2 * b + 5)
+            pack_m(b)
+            if b + 1 < BLOCKS:
+                regroup(2 * b + 6)
+                regroup(2 * b + 7)
+
+        for b in range(2):
+            for g in range(BLOCKS - 1):
+                for jt in range(BLOCKS * b, BLOCKS * (b + 1)):
+                    agg_pass(jt, g)
+        for jt in range(8):
+            agg_pass(jt, BLOCKS - 1)
+        for T in range(PACK * (BLOCKS - 1), TILES):
+            self_loop(T)
+        for u in range(BLOCKS * (BLOCKS - 1), BLOCKS * BLOCKS):
+            regroup(u)
+        for jt in range(8):
+            finish(jt)
+            if jt % 2 == 1:
+                quantise_unit(BLOCKS * (BLOCKS - 1) + jt // 2)
+        for jt in range(8, TILES):
+            for g in range(BLOCKS):
+                agg_pass(jt, g)
+        for jt in range(8, TILES):
+            finish(jt)

@@ -20,8 +20,9 @@ BLOCKS = NODES // (P * PACK)
 TILES = NODES // P
 UNIT = PACK * FEAT
 
-VECTOR_UNITS = (0, 2, 3, 4, 5, 7)
-GROUPED_SLOTS = 6
+VECTOR_UNITS = (0, 2, 3, 4, 5, 7, 8)
+REGROUP_IN_STEP = ((6,), (7, 8, 9, 10), (11,), (12, 13, 14, 15))
+GROUPED_SLOTS = {"vector": 3, "scalar": 4}
 RELU_ON_VECTOR_FROM = TILES - 2
 
 FLOPS = 2 * NODES * FEAT * FEAT + 2 * NODES * NODES * FEAT
@@ -40,12 +41,14 @@ def tile_gcnnodeclassifiernetwork_pa_kernel(tc, A, x, W1, b1, out):
         def bank(index, name):
             return psum.tile([P, FEAT], F32, tag="bank%d" % index, name=name)
 
-        grouped_made = []
+        grouped_made = {"vector": [], "scalar": []}
 
-        def new_grouped(name):
-            slot = len(grouped_made) % GROUPED_SLOTS
-            grouped_made.append(name)
-            return stage.tile([P, UNIT], BF16, tag="grouped%d" % slot, name=name, align_bytes=64)
+        def new_grouped(writer, name):
+            slot = len(grouped_made[writer]) % GROUPED_SLOTS[writer]
+            grouped_made[writer].append(name)
+            return stage.tile(
+                [P, UNIT], BF16, tag="grouped_%s%d" % (writer, slot), name=name, align_bytes=64
+            )
 
         def by_plane(tile_ap):
             return tile_ap.rearrange("p (t c i) -> p c t i", t=PACK, i=4)
@@ -125,10 +128,11 @@ def tile_gcnnodeclassifiernetwork_pa_kernel(tc, A, x, W1, b1, out):
                     )
 
         def regroup(u):
-            a_grouped[u] = new_grouped("a_grouped%d" % u)
             if u in VECTOR_UNITS:
+                a_grouped[u] = new_grouped("vector", "a_grouped%d" % u)
                 nc.vector.tensor_copy(out=by_word(a_grouped[u][:]), in_=by_plane(a_raw[u][:]))
             else:
+                a_grouped[u] = new_grouped("scalar", "a_grouped%d" % u)
                 nc.scalar.copy(out=by_word(a_grouped[u][:]), in_=by_plane(a_raw[u][:]))
 
         def quantise_unit(u):
@@ -153,7 +157,7 @@ def tile_gcnnodeclassifiernetwork_pa_kernel(tc, A, x, W1, b1, out):
                         )
 
         def copy_x(q):
-            x_grouped[q] = new_grouped("x_grouped%d" % q)
+            x_grouped[q] = new_grouped("scalar", "x_grouped%d" % q)
             words = x_grouped[q][:].bitcast(F32)
             for half in range(2):
                 nc.scalar.copy(
@@ -166,23 +170,27 @@ def tile_gcnnodeclassifiernetwork_pa_kernel(tc, A, x, W1, b1, out):
         def quantise_x(q):
             x_mx[q] = quantise("x%d" % q, x_grouped[q])
 
+        deg = {}
         d = {}
         h = {}
         m_f32 = {}
+        m_grouped = {}
         m_mx = {}
         self_term = {}
 
-        def inv_sqrt_degree(b):
-            deg = const.tile([P, BLOCKS], F32, name="deg%d" % b)
+        def sum_degree(b):
+            deg[b] = const.tile([P, BLOCKS], F32, name="deg%d" % b)
             nc.vector.tensor_reduce(
-                out=deg[:],
+                out=deg[b][:],
                 in_=sums[b][:, 0:64].rearrange("p (j r) -> p j r", r=16),
                 axis=AXIS.X,
                 op=ALU.add,
             )
+
+        def inv_sqrt(b):
             d[b] = const.tile([P, BLOCKS], F32, name="d%d" % b)
             nc.scalar.activation(
-                out=d[b][:], in_=deg[:], func=ACT.Abs_reciprocal_sqrt, bias=one[:, 0:1], scale=1.0
+                out=d[b][:], in_=deg[b][:], func=ACT.Abs_reciprocal_sqrt, bias=one[:, 0:1], scale=1.0
             )
 
         def d_of(T):
@@ -219,12 +227,14 @@ def tile_gcnnodeclassifiernetwork_pa_kernel(tc, A, x, W1, b1, out):
                 op1=ALU.add,
             )
 
-        def pack_m(g):
-            grouped = new_grouped("m_grouped%d" % g)
+        def regroup_m(g):
+            m_grouped[g] = new_grouped("vector", "m_grouped%d" % g)
             nc.vector.tensor_copy(
-                out=by_word(grouped[:]), in_=m_f32[g][:].rearrange("p t (c i) -> p c t i", i=4)
+                out=by_word(m_grouped[g][:]), in_=m_f32[g][:].rearrange("p t (c i) -> p c t i", i=4)
             )
-            m_mx[g] = quantise("m%d" % g, grouped)
+
+        def quantise_m(g):
+            m_mx[g] = quantise("m%d" % g, m_grouped[g])
 
         acc = {}
 
@@ -257,11 +267,11 @@ def tile_gcnnodeclassifiernetwork_pa_kernel(tc, A, x, W1, b1, out):
 
         column_sums(0)
         regroup(0)
-        quantise_unit(0)
         column_sums(1)
         regroup(1)
-        w_grouped = new_grouped("w_grouped")
+        w_grouped = new_grouped("vector", "w_grouped")
         nc.vector.tensor_copy(out=by_word(w_grouped[:]), in_=by_plane(w_raw[:]))
+        quantise_unit(0)
         w_mx = quantise("w", w_grouped)
         b_psum = bank(7, "b_psum")
         nc.tensor.matmul(out=b_psum[:], lhsT=ones[:], rhs=b_row[:], start=True, stop=True)
@@ -279,7 +289,8 @@ def tile_gcnnodeclassifiernetwork_pa_kernel(tc, A, x, W1, b1, out):
         column_sums(3)
         regroup(3)
 
-        inv_sqrt_degree(0)
+        sum_degree(0)
+        inv_sqrt(0)
         for T in range(PACK):
             h_pass(T)
         quantise_x(1)
@@ -290,18 +301,21 @@ def tile_gcnnodeclassifiernetwork_pa_kernel(tc, A, x, W1, b1, out):
             scale_rows(T)
         column_sums(4)
         regroup(4)
-        quantise_unit(4)
         quantise_x(2)
+        quantise_unit(4)
         transpose_x(3)
         copy_x(3)
         column_sums(5)
         regroup(5)
+        regroup_m(0)
         quantise_unit(5)
-        pack_m(0)
+        quantise_m(0)
         quantise_x(3)
         column_sums(6)
-        regroup(6)
+        for u in REGROUP_IN_STEP[0]:
+            regroup(u)
         column_sums(7)
+        sum_degree(1)
 
         for b in range(1, BLOCKS):
             for T in range(PACK * b, PACK * (b + 1)):
@@ -309,19 +323,19 @@ def tile_gcnnodeclassifiernetwork_pa_kernel(tc, A, x, W1, b1, out):
             if b + 1 < BLOCKS:
                 for u in range(BLOCKS * (b + 1), BLOCKS * (b + 2)):
                     column_sums(u)
-            inv_sqrt_degree(b)
+            inv_sqrt(b)
             for T in range(PACK * b, PACK * (b + 1)):
                 scale_rows(T)
             for T in range(PACK * (b - 1), PACK * b):
                 self_loop(T)
-            if b == 1:
-                regroup(7)
-            quantise_unit(2 * b + 4)
-            quantise_unit(2 * b + 5)
-            pack_m(b)
+            for u in REGROUP_IN_STEP[b]:
+                regroup(u)
             if b + 1 < BLOCKS:
-                regroup(2 * b + 6)
-                regroup(2 * b + 7)
+                sum_degree(b + 1)
+            regroup_m(b)
+            quantise_unit(2 * b + 4)
+            quantise_m(b)
+            quantise_unit(2 * b + 5)
 
         for b in range(2):
             for g in range(BLOCKS - 1):
@@ -331,12 +345,10 @@ def tile_gcnnodeclassifiernetwork_pa_kernel(tc, A, x, W1, b1, out):
             agg_pass(jt, BLOCKS - 1)
         for T in range(PACK * (BLOCKS - 1), TILES):
             self_loop(T)
-        for u in range(BLOCKS * (BLOCKS - 1), BLOCKS * BLOCKS):
-            regroup(u)
         for jt in range(8):
             finish(jt)
-            if jt % 2 == 1:
-                quantise_unit(BLOCKS * (BLOCKS - 1) + jt // 2)
+            if 3 <= jt < 3 + BLOCKS:
+                quantise_unit(BLOCKS * (BLOCKS - 1) + jt - 3)
         for jt in range(8, TILES):
             for g in range(BLOCKS):
                 agg_pass(jt, g)

from contextlib import ExitStack

import concourse.mybir as mybir
from concourse.masks import make_identity

BF16 = mybir.dt.bfloat16
F32 = mybir.dt.float32
U32 = mybir.dt.uint32
U8 = mybir.dt.uint8
FP8X4 = mybir.dt.float8_e4m3fn_x4
ACT = mybir.ActivationFunctionType
ALU = mybir.AluOpType
AXIS = mybir.AxisListType

P = 128
PACK = 4
NODES = 2048
FEAT = 512
BLOCKS = NODES // (P * PACK)
TILES = NODES // P
UNIT = PACK * FEAT

VECTOR_UNITS = (0, 2, 3, 4, 5, 7, 8)
REGROUP_IN_STEP = ((6,), (7, 8, 9, 10), (11,), (12, 13, 14, 15))
GROUPED_SLOTS = {"vector": 3, "scalar": 4}
RELU_ON_VECTOR_FROM = TILES - 2

FLOPS = 2 * NODES * FEAT * FEAT + 2 * NODES * NODES * FEAT


def tile_gcnnodeclassifiernetwork_pa_kernel(tc, A, x, W1, b1, out):
    nc = tc.nc
    with ExitStack() as ctx:
        ctx.enter_context(tc.manual_schedule())
        const = ctx.enter_context(tc.tile_pool(name="const", bufs=1))
        raw = ctx.enter_context(tc.tile_pool(name="raw", bufs=1))
        keep = ctx.enter_context(tc.tile_pool(name="keep", bufs=1))
        stage = ctx.enter_context(tc.tile_pool(name="stage", bufs=1))
        psum = ctx.enter_context(tc.psum_pool(name="psum", bufs=1))

        def bank(index, name):
            return psum.tile([P, FEAT], F32, tag="bank%d" % index, name=name)

        grouped_made = {"vector": [], "scalar": []}

        def new_grouped(writer, name):
            slot = len(grouped_made[writer]) % GROUPED_SLOTS[writer]
            grouped_made[writer].append(name)
            return stage.tile(
                [P, UNIT], BF16, tag="grouped_%s%d" % (writer, slot), name=name, align_bytes=64
            )

        def by_plane(tile_ap):
            return tile_ap.rearrange("p (t c i) -> p c t i", t=PACK, i=4)

        def by_word(tile_ap):
            return tile_ap.rearrange("p (c i t) -> p c t i", i=4, t=PACK)

        def quantise(name, grouped):
            codes = keep.tile([P, FEAT], U32, name=name + "_codes", align_bytes=64)
            scales = keep.tile([P, FEAT], U8, name=name + "_scales", align_bytes=64)
            nc.vector.quantize_mx(out=codes[:].bitcast(FP8X4), scales=scales[:], in_=grouped[:])
            return codes, scales

        b_row = const.tile([P, FEAT], BF16, name="b_row")
        nc.vector.memset(b_row[:], 0.0)
        one = const.tile([P, 1], F32, name="one")
        nc.vector.memset(one[:], 1.0)
        ones = const.tile([P, P], BF16, name="ones")
        nc.vector.memset(ones[:], 1.0)
        identity = const.tile([P, P], F32, name="identity")
        make_identity(nc, identity[:])
        warm = const.tile([P, 1], F32, name="warm")
        nc.scalar.activation(out=warm[:], in_=one[:], func=ACT.Abs_reciprocal_sqrt)

        a_rows = A.rearrange("(g t p) j -> g p t j", t=PACK, p=P)
        x_rows = x.rearrange("(T p) k -> p T k", p=P)
        a_raw = {}
        x_raw = {}

        def load_unit(u):
            b, g = divmod(u, BLOCKS)
            a_raw[u] = raw.tile([P, UNIT], BF16, name="a_raw%d" % u)
            nc.sync.dma_start(
                out=a_raw[u][:].rearrange("p (t j) -> p t j", t=PACK),
                in_=a_rows[g, :, :, FEAT * b : FEAT * (b + 1)],
            )

        def load_x(q):
            x_raw[q] = raw.tile([P, UNIT], BF16, name="x_raw%d" % q)
            nc.sync.dma_start(
                out=x_raw[q][:].rearrange("p (T k) -> p T k", T=PACK),
                in_=x_rows[:, PACK * q : PACK * (q + 1), :],
            )

        load_unit(0)
        load_unit(1)
        nc.sync.dma_start(out=b_row[0:1, :], in_=b1.rearrange("(o c) -> o c", o=1))
        w_raw = raw.tile([P, UNIT], BF16, name="w_raw")
        nc.sync.dma_start(
            out=w_raw[:].rearrange("q (u r) -> q u r", u=2),
            in_=W1.rearrange("(u q e) c -> q u (e c)", u=2, q=P, e=2),
        )
        for q in range(BLOCKS):
            load_x(q)
            load_unit(q + 2)
        for u in range(BLOCKS + 2, BLOCKS * BLOCKS):
            load_unit(u)

        sums = {}
        a_grouped = {}
        a_mx = {}

        def column_sums(u):
            b, g = divmod(u, BLOCKS)
            if g == 0:
                sums[b] = bank(6 + b % 2, "sums%d" % b)
            for jl in range(BLOCKS):
                for t in range(PACK):
                    col = 16 * jl + PACK * g + t
                    src = FEAT * t + P * jl
                    nc.tensor.matmul(
                        out=sums[b][:, col : col + 1],
                        lhsT=a_raw[u][:, src : src + P],
                        rhs=ones[:, 0:1],
                        start=True,
                        stop=True,
                    )

        def regroup(u):
            if u in VECTOR_UNITS:
                a_grouped[u] = new_grouped("vector", "a_grouped%d" % u)
                nc.vector.tensor_copy(out=by_word(a_grouped[u][:]), in_=by_plane(a_raw[u][:]))
            else:
                a_grouped[u] = new_grouped("scalar", "a_grouped%d" % u)
                nc.scalar.copy(out=by_word(a_grouped[u][:]), in_=by_plane(a_raw[u][:]))

        def quantise_unit(u):
            a_mx[u] = quantise("a%d" % u, a_grouped[u])

        x_t = {}
        x_grouped = {}
        x_mx = {}

        def transpose_x(q):
            words = x_raw[q][:].bitcast(F32)
            for half in range(2):
                x_t[(q, half)] = bank(4 + half, "x_t%d_%d" % (q, half))
                for tl in range(2):
                    for u in range(2):
                        src = 256 * (2 * half + tl) + P * u
                        dst = P * (2 * tl + u)
                        nc.tensor.transpose(
                            out=x_t[(q, half)][:, dst : dst + P],
                            in_=words[:, src : src + P],
                            identity=identity[:],
                        )

        def copy_x(q):
            x_grouped[q] = new_grouped("scalar", "x_grouped%d" % q)
            words = x_grouped[q][:].bitcast(F32)
            for half in range(2):
                nc.scalar.copy(
                    out=words[:, FEAT * half : FEAT * (half + 1)].rearrange(
                        "p (T r u) -> p T r u", T=2, u=2
                    ),
                    in_=x_t[(q, half)][:].rearrange("p (T u r) -> p T r u", T=2, u=2),
                )

        def quantise_x(q):
            x_mx[q] = quantise("x%d" % q, x_grouped[q])

        deg = {}
        d = {}
        h = {}
        m_f32 = {}
        m_grouped = {}
        m_mx = {}
        self_term = {}

        def sum_degree(b):
            deg[b] = const.tile([P, BLOCKS], F32, name="deg%d" % b)
            nc.vector.tensor_reduce(
                out=deg[b][:],
                in_=sums[b][:, 0:64].rearrange("p (j r) -> p j r", r=16),
                axis=AXIS.X,
                op=ALU.add,
            )

        def inv_sqrt(b):
            d[b] = const.tile([P, BLOCKS], F32, name="d%d" % b)
            nc.scalar.activation(
                out=d[b][:], in_=deg[b][:], func=ACT.Abs_reciprocal_sqrt, bias=one[:, 0:1], scale=1.0
            )

        def d_of(T):
            return d[T // BLOCKS][:, T % BLOCKS : T % BLOCKS + 1]

        def h_pass(T):
            q, r = divmod(T, PACK)
            h[T] = bank(T % 4, "h%d" % T)
            nc.tensor.matmul_mx(
                out=h[T][:],
                lhsT=x_mx[q][0][:, P * r : P * (r + 1)].bitcast(FP8X4),
                lhsT_scale=x_mx[q][1][:, P * r : P * (r + 1)],
                rhs=w_mx[0][:].bitcast(FP8X4),
                rhs_scale=w_mx[1][:],
                start=True,
                stop=True,
            )

        def scale_rows(T):
            g, t = divmod(T, PACK)
            if t == 0:
                m_f32[g] = stage.tile([P, PACK, FEAT], F32, tag="m_f32_%d" % (g % 2), name="m_f32_%d" % g)
            nc.scalar.activation(out=m_f32[g][:, t, :], in_=h[T][:], func=ACT.Copy, scale=d_of(T))

        def self_loop(T):
            g, t = divmod(T, PACK)
            self_term[T] = keep.tile([P, FEAT], F32, name="self_term%d" % T)
            nc.vector.scalar_tensor_tensor(
                out=self_term[T][:],
                in0=m_f32[g][:, t, :],
                scalar=d_of(T),
                in1=b_all[:],
                op0=ALU.mult,
                op1=ALU.add,
            )

        def regroup_m(g):
            m_grouped[g] = new_grouped("vector", "m_grouped%d" % g)
            nc.vector.tensor_copy(
                out=by_word(m_grouped[g][:]), in_=m_f32[g][:].rearrange("p t (c i) -> p c t i", i=4)
            )

        def quantise_m(g):
            m_mx[g] = quantise("m%d" % g, m_grouped[g])

        acc = {}

        def agg_pass(jt, g):
            b, jl = divmod(jt, BLOCKS)
            if g == 0:
                acc[jt] = bank((jt + 4) % 8, "acc%d" % jt)
            codes, scales = a_mx[BLOCKS * b + g]
            nc.tensor.matmul_mx(
                out=acc[jt][:],
                lhsT=codes[:, P * jl : P * (jl + 1)].bitcast(FP8X4),
                lhsT_scale=scales[:, P * jl : P * (jl + 1)],
                rhs=m_mx[g][0][:].bitcast(FP8X4),
                rhs_scale=m_mx[g][1][:],
                start=(g == 0),
                stop=(g == BLOCKS - 1),
            )

        def finish(jt):
            res = self_term[jt]
            nc.vector.scalar_tensor_tensor(
                out=res[:], in0=acc[jt][:], scalar=d_of(jt), in1=res[:], op0=ALU.mult, op1=ALU.add
            )
            if jt >= RELU_ON_VECTOR_FROM:
                nc.vector.tensor_scalar_max(out=res[:], in0=res[:], scalar1=0.0)
            else:
                nc.scalar.activation(out=res[:], in_=res[:], func=ACT.Relu)
            nc.sync.dma_start(out=out[P * jt : P * (jt + 1), :], in_=res[:])


        column_sums(0)
        regroup(0)
        column_sums(1)
        regroup(1)
        w_grouped = new_grouped("vector", "w_grouped")
        nc.vector.tensor_copy(out=by_word(w_grouped[:]), in_=by_plane(w_raw[:]))
        quantise_unit(0)
        w_mx = quantise("w", w_grouped)
        b_psum = bank(7, "b_psum")
        nc.tensor.matmul(out=b_psum[:], lhsT=ones[:], rhs=b_row[:], start=True, stop=True)
        b_all = const.tile([P, FEAT], F32, name="b_all")
        nc.scalar.copy(out=b_all[:], in_=b_psum[:])
        transpose_x(0)
        copy_x(0)
        quantise_unit(1)
        column_sums(2)
        regroup(2)
        quantise_x(0)
        quantise_unit(2)
        transpose_x(1)
        copy_x(1)
        column_sums(3)
        regroup(3)

        sum_degree(0)
        inv_sqrt(0)
        for T in range(PACK):
            h_pass(T)
        quantise_x(1)
        quantise_unit(3)
        transpose_x(2)
        copy_x(2)
        for T in range(PACK):
            scale_rows(T)
        column_sums(4)
        regroup(4)
        quantise_x(2)
        quantise_unit(4)
        transpose_x(3)
        copy_x(3)
        column_sums(5)
        regroup(5)
        regroup_m(0)
        quantise_unit(5)
        quantise_m(0)
        quantise_x(3)
        column_sums(6)
        for u in REGROUP_IN_STEP[0]:
            regroup(u)
        column_sums(7)
        sum_degree(1)

        for b in range(1, BLOCKS):
            for T in range(PACK * b, PACK * (b + 1)):
                h_pass(T)
            if b + 1 < BLOCKS:
                for u in range(BLOCKS * (b + 1), BLOCKS * (b + 2)):
                    column_sums(u)
            inv_sqrt(b)
            for T in range(PACK * b, PACK * (b + 1)):
                scale_rows(T)
            for T in range(PACK * (b - 1), PACK * b):
                self_loop(T)
            for u in REGROUP_IN_STEP[b]:
                regroup(u)
            if b + 1 < BLOCKS:
                sum_degree(b + 1)
            regroup_m(b)
            quantise_unit(2 * b + 4)
            quantise_m(b)
            quantise_unit(2 * b + 5)

        for b in range(2):
            for g in range(BLOCKS - 1):
                for jt in range(BLOCKS * b, BLOCKS * (b + 1)):
                    agg_pass(jt, g)
        for jt in range(8):
            agg_pass(jt, BLOCKS - 1)
        for T in range(PACK * (BLOCKS - 1), TILES):
            self_loop(T)
        for jt in range(8):
            finish(jt)
            if 3 <= jt < 3 + BLOCKS:
                quantise_unit(BLOCKS * (BLOCKS - 1) + jt - 3)
        for jt in range(8, TILES):
            for g in range(BLOCKS):
                agg_pass(jt, g)
        for jt in range(8, TILES):
            finish(jt)
